import numpy as np
import ml_dtypes


def mxq(x, axis, fmt="e4m3"):
    dtype, down = {"e4m3": (ml_dtypes.float8_e4m3fn, 7), "e5m2": (ml_dtypes.float8_e5m2, 14)}[fmt]
    v = np.moveaxis(np.asarray(x, np.float32).astype(ml_dtypes.bfloat16).astype(np.float64), axis, -1)
    blocks = v.reshape(v.shape[:-1] + (-1, 32))
    amax = np.abs(blocks).max(-1, keepdims=True)
    byte = np.maximum(np.where(amax > 0, np.frexp(amax)[1] - 1 + 127, 0) - down, 1)
    scale = np.exp2(byte - 127.0)
    codes = (blocks / scale).astype(np.float32).astype(dtype).astype(np.float64)
    return np.moveaxis((codes * scale).reshape(v.shape), -1, axis)


WIDE = False


def mx_kscale(k):
    if not WIDE:
        return np.ones(k)
    levels = np.array([10, -10, 5, -5, 0])
    if k % 512:
        return np.exp2(np.random.permutation(np.resize(levels, k // 32))).repeat(32)
    a = np.empty((k // 512, 16))
    for p in range(k // 512):
        a[p, :8] = np.random.permutation(np.resize(levels, 8))
        for g in range(8):
            far = levels[np.abs(levels - a[p, g]) >= 10]
            a[p, g + 8] = far[np.random.randint(len(far))]
    return np.exp2(a.ravel()).repeat(32)


BF16 = ml_dtypes.bfloat16


def bf(x):
    return np.asarray(x, np.float32).astype(BF16)


def f64(x):
    return np.asarray(x).astype(np.float64)


B, S, D, H, HD, FF = 1, 512, 2048, 16, 128, 8192
EPS = 1e-05


def layer_norm(x, scale, bias):
    mu = x.mean(-1, keepdims=True)
    var = x.var(-1, keepdims=True)
    return (x - mu) / np.sqrt(var + EPS) * scale + bias


def setup_inputs():
    s = mx_kscale(D)
    return {
        "x": bf(np.random.standard_normal((B, S, D)) + 0.5 * np.random.standard_normal((B, S, 1))),
        "ln1_s": bf((1.0 + 0.1 * np.random.standard_normal(D)) * s),
        "ln1_b": bf(0.1 * np.random.standard_normal(D) * s),
        "wq_k": bf(np.random.standard_normal((D, H, HD)) / np.sqrt(D) / s[:, None, None]),
        "wq_b": bf(0.1 * np.random.standard_normal((H, HD))),
        "wk_k": bf(np.random.standard_normal((D, HD)) / np.sqrt(D) / s[:, None]),
        "wk_b": bf(0.1 * np.random.standard_normal(HD)),
        "wv_k": bf(np.random.standard_normal((D, HD)) / np.sqrt(D) / s[:, None]),
        "wv_b": bf(0.1 * np.random.standard_normal(HD)),
    }


def reference(x, ln1_s, ln1_b, wq_k, wq_b, wk_k, wk_b, wv_k, wv_b):
    h = layer_norm(f64(x), f64(ln1_s), f64(ln1_b))
    hq = mxq(h, 2, "e4m3")
    q = (hq @ mxq(f64(wq_k).reshape(D, H * HD), 0, "e4m3")).reshape(B, S, H, HD) + f64(wq_b)
    k = (hq @ mxq(f64(wk_k), 0, "e4m3")) + f64(wk_b)
    v = (hq @ mxq(f64(wv_k), 0, "e4m3")) + f64(wv_b)
    return q, k, v

@@ -1,0 +1,258 @@
+from contextlib import ExitStack
+
+import concourse.mybir as mybir
+from concourse.masks import make_identity
+
+F32 = mybir.dt.float32
+BF16 = mybir.dt.bfloat16
+U32 = mybir.dt.uint32
+U8 = mybir.dt.uint8
+FP8X4 = mybir.dt.float8_e4m3fn_x4
+ALU = mybir.AluOpType
+ACT = mybir.ActivationFunctionType
+
+P = 128
+PACK = 4
+TOKENS = 512
+D = 2048
+Q_COLS = 2048
+HEAD = 128
+EPS = 1e-05
+
+TOKEN_TILES = TOKENS // P
+D_SQUARES = D // P
+PASSES = D // (P * PACK)
+BANK = 512
+BANKS = 8
+STATS_CHUNK = 512
+CHUNKS = D // STATS_CHUNK
+RUN = 4
+
+Q_BLOCKS = Q_COLS // BANK
+BLOCKS = Q_BLOCKS + 1
+PIECES = BLOCKS * PASSES
+EARLY_SCALAR = PASSES
+EARLY_PIECES = 2 * PASSES
+AHEAD = 2
+GROUPED_BUFS = 8
+LOADED_BUFS = 12
+BIAS_AFTER_PIECE = 12
+
+FLOPS = 2 * TOKENS * D * (Q_COLS + 2 * HEAD)
+
+
+def tile_transformerlayer_pa_kernel(
+    tc, x, ln1_s, ln1_b, wq_k, wq_b, wk_k, wk_b, wv_k, wv_b, out_0, out_1, out_2
+):
+    nc = tc.nc
+
+    x_tiles = x.rearrange("b (i p) d -> (b i) p d", p=P)
+    wq_rows = wq_k.rearrange("(g p t) h e -> g p t (h e)", p=P, t=PACK)
+    wk_rows = wk_k.rearrange("(g p t) e -> g p t e", p=P, t=PACK)
+    wv_rows = wv_k.rearrange("(g p t) e -> g p t e", p=P, t=PACK)
+    q_tiles = out_0.rearrange("b (i p) h e -> (b i) p (h e)", p=P)
+    k_tiles = out_1.rearrange("b (i p) e -> (b i) p e", p=P)
+    v_tiles = out_2.rearrange("b (i p) e -> (b i) p e", p=P)
+
+    with ExitStack() as ctx:
+        ctx.enter_context(tc.manual_schedule())
+        keep = ctx.enter_context(tc.tile_pool(name="keep", bufs=1))
+        small = ctx.enter_context(tc.tile_pool(name="small", bufs=TOKEN_TILES))
+        loaded = ctx.enter_context(tc.tile_pool(name="loaded", bufs=LOADED_BUFS))
+        stage = ctx.enter_context(tc.tile_pool(name="stage", bufs=GROUPED_BUFS))
+        h_stage = ctx.enter_context(tc.tile_pool(name="h_stage", bufs=2))
+        quantised = ctx.enter_context(tc.tile_pool(name="quantised", bufs=3))
+        results = ctx.enter_context(tc.tile_pool(name="results", bufs=6))
+        psum = ctx.enter_context(tc.psum_pool(name="psum", bufs=BANKS))
+
+        identity = keep.tile([P, P], F32, name="identity")
+        make_identity(nc, identity[:])
+        minus_half = keep.tile([P, 1], F32, name="minus_half")
+        nc.vector.memset(minus_half[:], -0.5)
+
+        gain_raw = keep.tile([P, 2, PASSES, PACK], BF16, name="gain_raw")
+        nc.scalar.dma_start(out=gain_raw[:, 0, :, :], in_=ln1_s.rearrange("(g p t) -> p g t", p=P, t=PACK))
+        nc.scalar.dma_start(out=gain_raw[:, 1, :, :], in_=ln1_b.rearrange("(g p t) -> p g t", p=P, t=PACK))
+        gain_cols = keep.tile([P, 2 * D_SQUARES], F32, name="gain_cols")
+        nc.scalar.copy(out=gain_cols[:], in_=gain_raw[:].rearrange("p s g t -> p (s g t)"))
+
+        piece_rows = []
+
+        def load_piece():
+            b, g = divmod(len(piece_rows), PASSES)
+            rows = loaded.tile([P, PACK, BANK], BF16, name="rows")
+            if b < Q_BLOCKS:
+                nc.sync.dma_start(out=rows[:], in_=wq_rows[g][:, :, BANK * b : BANK * (b + 1)])
+                piece_rows.append(rows[:])
+            else:
+                nc.sync.dma_start(out=rows[:, :, 0:HEAD], in_=wk_rows[g])
+                nc.sync.dma_start(out=rows[:, :, HEAD : 2 * HEAD], in_=wv_rows[g])
+                piece_rows.append(rows[:, :, 0 : 2 * HEAD])
+
+        x_sb = []
+        for i in range(TOKEN_TILES):
+            x_i = keep.tile([P, D], BF16, name="x%d" % i)
+            nc.sync.dma_start(out=x_i[:], in_=x_tiles[i])
+            x_sb.append(x_i)
+            load_piece()
+        bias_all = keep.tile([P, Q_COLS + 2 * HEAD], BF16, name="bias_all")
+        for u in range(TOKEN_TILES, PIECES):
+            load_piece()
+            if u == BIAS_AFTER_PIECE:
+                nc.sync.dma_start(
+                    out=bias_all[:, 0:Q_COLS], in_=wq_b.rearrange("h e -> (h e)").partition_broadcast(P)
+                )
+                nc.sync.dma_start(out=bias_all[:, Q_COLS : Q_COLS + HEAD], in_=wk_b.partition_broadcast(P))
+                nc.sync.dma_start(out=bias_all[:, Q_COLS + HEAD :], in_=wv_b.partition_broadcast(P))
+
+        def regroup(pool, copy, rows):
+            width = rows.shape[2]
+            grouped = pool.tile([P, BANK, PACK], BF16, align_bytes=64, name="grouped")
+            copy(
+                out=grouped[:, :width, :].rearrange("p (c i) t -> p c t i", i=RUN),
+                in_=rows.rearrange("p t (c i) -> p c t i", i=RUN),
+            )
+            return grouped[:, :width, :].rearrange("p w t -> p (w t)")
+
+        def quantise(grouped, codes, scales):
+            nc.vector.quantize_mx(out=codes.bitcast(FP8X4), scales=scales, in_=grouped)
+
+        piece_grouped = {}
+        block_codes = {}
+        block_scales = {}
+
+        def regroup_piece(u, copy):
+            piece_grouped[u] = regroup(stage, copy, piece_rows[u])
+
+        def quantise_piece(u):
+            b, g = divmod(u, PASSES)
+            if g == 0:
+                block_codes[b] = quantised.tile([P, PASSES, BANK], U32, name="w_codes", align_bytes=64)
+                block_scales[b] = quantised.tile([P, PASSES, BANK], U8, name="w_scales", align_bytes=64)
+            width = piece_rows[u].shape[2]
+            quantise(piece_grouped[u], block_codes[b][:, g, :width], block_scales[b][:, g, :width])
+
+        for u in range(EARLY_SCALAR):
+            regroup_piece(u, nc.scalar.copy)
+
+        stats = [small.tile([P, CHUNKS, 6], F32, name="stats") for i in range(TOKEN_TILES)]
+        mean_var = [small.tile([P, 2], F32, name="mean_var") for i in range(TOKEN_TILES)]
+        normed = [keep.tile([P, D], F32, name="normed%d" % i) for i in range(TOKEN_TILES)]
+
+        def in_order(x_i):
+            return x_i[:].rearrange("p (g q t) -> p g t q", q=P, t=PACK)
+
+        def in_squares(normed_i):
+            return normed_i[:].rearrange("p (g t q) -> p g t q", q=P, t=PACK)
+
+        def normalise(i):
+            var_eps = small.tile([P, 1], F32, name="var_eps")
+            nc.vector.tensor_scalar_add(out=var_eps[:], in0=mean_var[i][:, 1:2], scalar1=EPS)
+            minus_mean = small.tile([P, 1], F32, name="minus_mean")
+            nc.vector.tensor_scalar_mul(out=minus_mean[:], in0=mean_var[i][:, 0:1], scalar1=-1.0)
+            rstd = small.tile([P, 1], F32, name="rstd")
+            nc.gpsimd.tensor_tensor(out=rstd[:], in0=var_eps[:], in1=minus_half[:], op=ALU.pow)
+            if i < TOKEN_TILES - 1:
+                nc.gpsimd.tensor_scalar(
+                    out=in_squares(normed[i]),
+                    in0=in_order(x_sb[i]),
+                    scalar1=minus_mean[:],
+                    scalar2=rstd[:],
+                    op0=ALU.add,
+                    op1=ALU.mult,
+                )
+            else:
+                shift = small.tile([P, 1], F32, name="shift")
+                nc.vector.tensor_mul(out=shift[:], in0=minus_mean[:], in1=rstd[:])
+                nc.scalar.activation(
+                    out=in_squares(normed[i]),
+                    in_=in_order(x_sb[i]),
+                    func=ACT.Identity,
+                    scale=rstd[:],
+                    bias=shift[:],
+                )
+
+        for i in range(TOKEN_TILES + 1):
+            for c in range(CHUNKS):
+                if i < TOKEN_TILES:
+                    nc.vector.bn_stats(
+                        out=stats[i][:, c, :], in_=x_sb[i][:, STATS_CHUNK * c : STATS_CHUNK * (c + 1)]
+                    )
+                if i > 0 and c == 0:
+                    nc.vector.bn_aggr(out=mean_var[i - 1][:], in_=stats[i - 1][:].rearrange("p c s -> p (c s)"))
+                if i > 0 and c == 1:
+                    normalise(i - 1)
+
+        for u in range(EARLY_SCALAR, EARLY_PIECES):
+            regroup_piece(u, nc.vector.tensor_copy)
+        for u in range(EARLY_SCALAR, EARLY_PIECES):
+            quantise_piece(u)
+
+        h_rows = keep.tile([P, D_SQUARES, TOKENS], BF16, name="h_rows")
+        h_codes = keep.tile([P, PASSES, TOKENS], U32, name="h_codes", align_bytes=64)
+        h_scales = keep.tile([P, PASSES, TOKENS], U8, name="h_scales", align_bytes=64)
+        for g in range(PASSES):
+            for j in range(PACK * g, PACK * (g + 1)):
+                square = psum.tile([P, BANK], F32, tag="bank", name="square")
+                for i in range(TOKEN_TILES):
+                    nc.tensor.transpose(
+                        square[:, P * i : P * (i + 1)], normed[i][:, P * j : P * (j + 1)], identity[:]
+                    )
+                nc.scalar.activation(
+                    out=h_rows[:, j, :],
+                    in_=square[:],
+                    func=ACT.Identity,
+                    scale=gain_cols[:, j : j + 1],
+                    bias=gain_cols[:, D_SQUARES + j : D_SQUARES + j + 1],
+                )
+            h_grouped = regroup(h_stage, nc.vector.tensor_copy, h_rows[:, PACK * g : PACK * (g + 1), :])
+            quantise_piece(g)
+            quantise(h_grouped, h_codes[:, g, :], h_scales[:, g, :])
+
+        block_sums = {}
+
+        def multiply_piece(u):
+            b, g = divmod(u, PASSES)
+            width = piece_rows[u].shape[2]
+            if g == 0:
+                block_sums[b] = [
+                    psum.tile([P, BANK], F32, tag="bank", name="sums%d" % i) for i in range(TOKEN_TILES)
+                ]
+            for i in range(TOKEN_TILES):
+                nc.tensor.matmul_mx(
+                    out=block_sums[b][i][:, :width],
+                    lhsT=h_codes[:, g, P * i : P * (i + 1)].bitcast(FP8X4),
+                    lhsT_scale=h_scales[:, g, P * i : P * (i + 1)],
+                    rhs=block_codes[b][:, g, :width].bitcast(FP8X4),
+                    rhs_scale=block_scales[b][:, g, :width],
+                    start=(g == 0),
+                    stop=(g == PASSES - 1),
+                )
+
+        def finish_block(b):
+            width = piece_rows[PASSES * b].shape[2]
+            for i in range(TOKEN_TILES):
+                result = results.tile([P, BANK], F32, name="result")
+                nc.vector.tensor_tensor(
+                    out=result[:, :width],
+                    in0=block_sums[b][i][:, :width],
+                    in1=bias_all[:, BANK * b : BANK * b + width],
+                    op=ALU.add,
+                )
+                if b < Q_BLOCKS:
+                    nc.sync.dma_start(out=q_tiles[i][:, BANK * b : BANK * (b + 1)], in_=result[:])
+                else:
+                    nc.sync.dma_start(out=k_tiles[i], in_=result[:, 0:HEAD])
+                    nc.sync.dma_start(out=v_tiles[i], in_=result[:, HEAD : 2 * HEAD])
+
+        for u in range(PIECES):
+            b, g = divmod(u, PASSES)
+            ahead = u + AHEAD
+            if EARLY_PIECES <= ahead < PIECES:
+                regroup_piece(ahead, nc.vector.tensor_copy if ahead % PASSES == 0 else nc.scalar.copy)
+            if u >= EARLY_PIECES:
+                quantise_piece(u)
+            multiply_piece(u)
+            if g == 2 and b > 0:
+                finish_block(b - 1)
+        finish_block(BLOCKS - 1)

@@ -23,7 +23,7 @@ TOKEN_TILES = TOKENS // P
 D_SQUARES = D // P
 PASSES = D // (P * PACK)
 BANK = 512
-BANKS = 8
+BF16_BANK = 2 * BANK
 STATS_CHUNK = 512
 CHUNKS = D // STATS_CHUNK
 RUN = 4
@@ -31,12 +31,10 @@ RUN = 4
 Q_BLOCKS = Q_COLS // BANK
 BLOCKS = Q_BLOCKS + 1
 PIECES = BLOCKS * PASSES
-EARLY_SCALAR = PASSES
-EARLY_PIECES = 2 * PASSES
-AHEAD = 2
+AHEAD = 3
 GROUPED_BUFS = 8
-LOADED_BUFS = 12
-BIAS_AFTER_PIECE = 12
+LOADED_BUFS = 16
+BIAS_AFTER_PIECE = 11
 
 FLOPS = 2 * TOKENS * D * (Q_COLS + 2 * HEAD)
 
@@ -63,18 +61,17 @@ def tile_transformerlayer_pa_kernel(
         h_stage = ctx.enter_context(tc.tile_pool(name="h_stage", bufs=2))
         quantised = ctx.enter_context(tc.tile_pool(name="quantised", bufs=3))
         results = ctx.enter_context(tc.tile_pool(name="results", bufs=6))
-        psum = ctx.enter_context(tc.psum_pool(name="psum", bufs=BANKS))
+        even_sums = ctx.enter_context(tc.psum_pool(name="even_sums", bufs=TOKEN_TILES))
+        shared_banks = ctx.enter_context(tc.psum_pool(name="shared_banks", bufs=TOKEN_TILES))
 
-        identity = keep.tile([P, P], F32, name="identity")
-        make_identity(nc, identity[:])
         minus_half = keep.tile([P, 1], F32, name="minus_half")
         nc.vector.memset(minus_half[:], -0.5)
-
-        gain_raw = keep.tile([P, 2, PASSES, PACK], BF16, name="gain_raw")
-        nc.scalar.dma_start(out=gain_raw[:, 0, :, :], in_=ln1_s.rearrange("(g p t) -> p g t", p=P, t=PACK))
-        nc.scalar.dma_start(out=gain_raw[:, 1, :, :], in_=ln1_b.rearrange("(g p t) -> p g t", p=P, t=PACK))
-        gain_cols = keep.tile([P, 2 * D_SQUARES], F32, name="gain_cols")
-        nc.scalar.copy(out=gain_cols[:], in_=gain_raw[:].rearrange("p s g t -> p (s g t)"))
+        warm = keep.tile([P, 1], F32, name="warm")
+        nc.scalar.activation(out=warm[:], in_=minus_half[:], func=ACT.Identity)
+        identity = keep.tile([P, P], F32, name="identity")
+        make_identity(nc, identity[:])
+        identity_bf16 = keep.tile([P, P], BF16, name="identity_bf16")
+        nc.vector.tensor_copy(out=identity_bf16[:], in_=identity[:])
 
         piece_rows = []
 
@@ -95,6 +92,9 @@ def tile_transformerlayer_pa_kernel(
             nc.sync.dma_start(out=x_i[:], in_=x_tiles[i])
             x_sb.append(x_i)
             load_piece()
+        gain_raw = keep.tile([P, 2, PASSES, PACK], BF16, name="gain_raw")
+        nc.sync.dma_start(out=gain_raw[:, 0, :, :], in_=ln1_s.rearrange("(g p t) -> p g t", p=P, t=PACK))
+        nc.sync.dma_start(out=gain_raw[:, 1, :, :], in_=ln1_b.rearrange("(g p t) -> p g t", p=P, t=PACK))
         bias_all = keep.tile([P, Q_COLS + 2 * HEAD], BF16, name="bias_all")
         for u in range(TOKEN_TILES, PIECES):
             load_piece()
@@ -124,6 +124,24 @@ def tile_transformerlayer_pa_kernel(
         def regroup_piece(u, copy):
             piece_grouped[u] = regroup(stage, copy, piece_rows[u])
 
+        def regroup_piece_via_tensor(u):
+            grouped = stage.tile([P, BANK, PACK], BF16, align_bytes=64, name="grouped")
+            flat = grouped[:].rearrange("p w t -> p (w t)")
+            columns = BANK // PACK
+            for half in range(2):
+                bank = shared_banks.tile([P, BF16_BANK], BF16, tag="bank", name="bank")
+                for c in range(2):
+                    first = columns * (2 * half + c)
+                    nc.tensor.matmul(
+                        out=bank[:, BANK * c : BANK * (c + 1)].rearrange("p (w t) -> p w t", t=PACK),
+                        lhsT=identity_bf16[:],
+                        rhs=piece_rows[u][:, :, first : first + columns].rearrange("p t w -> p w t"),
+                        start=True,
+                        stop=True,
+                    )
+                nc.scalar.copy(out=flat[:, BF16_BANK * half : BF16_BANK * (half + 1)], in_=bank[:])
+            piece_grouped[u] = flat
+
         def quantise_piece(u):
             b, g = divmod(u, PASSES)
             if g == 0:
@@ -132,82 +150,62 @@ def tile_transformerlayer_pa_kernel(
             width = piece_rows[u].shape[2]
             quantise(piece_grouped[u], block_codes[b][:, g, :width], block_scales[b][:, g, :width])
 
-        for u in range(EARLY_SCALAR):
-            regroup_piece(u, nc.scalar.copy)
-
         stats = [small.tile([P, CHUNKS, 6], F32, name="stats") for i in range(TOKEN_TILES)]
         mean_var = [small.tile([P, 2], F32, name="mean_var") for i in range(TOKEN_TILES)]
+        minus_mean = [small.tile([P, 1], F32, name="minus_mean") for i in range(TOKEN_TILES)]
+        rstd = [small.tile([P, 1], F32, name="rstd") for i in range(TOKEN_TILES)]
         normed = [keep.tile([P, D], F32, name="normed%d" % i) for i in range(TOKEN_TILES)]
 
-        def in_order(x_i):
-            return x_i[:].rearrange("p (g q t) -> p g t q", q=P, t=PACK)
+        def take_stats(i, chunks):
+            for c in chunks:
+                nc.vector.bn_stats(
+                    out=stats[i][:, c, :], in_=x_sb[i][:, STATS_CHUNK * c : STATS_CHUNK * (c + 1)]
+                )
 
-        def in_squares(normed_i):
-            return normed_i[:].rearrange("p (g t q) -> p g t q", q=P, t=PACK)
+        def aggregate(i):
+            nc.vector.bn_aggr(out=mean_var[i][:], in_=stats[i][:].rearrange("p c s -> p (c s)"))
 
-        def normalise(i):
+        def take_rstd(i):
             var_eps = small.tile([P, 1], F32, name="var_eps")
             nc.vector.tensor_scalar_add(out=var_eps[:], in0=mean_var[i][:, 1:2], scalar1=EPS)
-            minus_mean = small.tile([P, 1], F32, name="minus_mean")
-            nc.vector.tensor_scalar_mul(out=minus_mean[:], in0=mean_var[i][:, 0:1], scalar1=-1.0)
-            rstd = small.tile([P, 1], F32, name="rstd")
-            nc.gpsimd.tensor_tensor(out=rstd[:], in0=var_eps[:], in1=minus_half[:], op=ALU.pow)
+            nc.vector.tensor_scalar_mul(out=minus_mean[i][:], in0=mean_var[i][:, 0:1], scalar1=-1.0)
+            nc.gpsimd.tensor_tensor(out=rstd[i][:], in0=var_eps[:], in1=minus_half[:], op=ALU.pow)
+
+        def normalise(i, engine):
+            engine.tensor_scalar(
+                out=normed[i][:].rearrange("p (g t q) -> p g t q", q=P, t=PACK),
+                in0=x_sb[i][:].rearrange("p (g q t) -> p g t q", q=P, t=PACK),
+                scalar1=minus_mean[i][:],
+                scalar2=rstd[i][:],
+                op0=ALU.add,
+                op1=ALU.mult,
+            )
+
+        take_stats(0, range(CHUNKS))
+        regroup_piece(0, nc.scalar.copy)
+        regroup_piece(1, nc.scalar.copy)
+        regroup_piece_via_tensor(2)
+        regroup_piece_via_tensor(3)
+        regroup_piece_via_tensor(4)
+        for i in range(1, TOKEN_TILES):
+            take_stats(i, range(1))
+            aggregate(i - 1)
+            take_stats(i, range(1, 2))
+            take_rstd(i - 1)
             if i < TOKEN_TILES - 1:
-                nc.gpsimd.tensor_scalar(
-                    out=in_squares(normed[i]),
-                    in0=in_order(x_sb[i]),
-                    scalar1=minus_mean[:],
-                    scalar2=rstd[:],
-                    op0=ALU.add,
-                    op1=ALU.mult,
-                )
-            else:
-                shift = small.tile([P, 1], F32, name="shift")
-                nc.vector.tensor_mul(out=shift[:], in0=minus_mean[:], in1=rstd[:])
-                nc.scalar.activation(
-                    out=in_squares(normed[i]),
-                    in_=in_order(x_sb[i]),
-                    func=ACT.Identity,
-                    scale=rstd[:],
-                    bias=shift[:],
-                )
-
-        for i in range(TOKEN_TILES + 1):
-            for c in range(CHUNKS):
-                if i < TOKEN_TILES:
-                    nc.vector.bn_stats(
-                        out=stats[i][:, c, :], in_=x_sb[i][:, STATS_CHUNK * c : STATS_CHUNK * (c + 1)]
-                    )
-                if i > 0 and c == 0:
-                    nc.vector.bn_aggr(out=mean_var[i - 1][:], in_=stats[i - 1][:].rearrange("p c s -> p (c s)"))
-                if i > 0 and c == 1:
-                    normalise(i - 1)
-
-        for u in range(EARLY_SCALAR, EARLY_PIECES):
-            regroup_piece(u, nc.vector.tensor_copy)
-        for u in range(EARLY_SCALAR, EARLY_PIECES):
-            quantise_piece(u)
-
-        h_rows = keep.tile([P, D_SQUARES, TOKENS], BF16, name="h_rows")
-        h_codes = keep.tile([P, PASSES, TOKENS], U32, name="h_codes", align_bytes=64)
-        h_scales = keep.tile([P, PASSES, TOKENS], U8, name="h_scales", align_bytes=64)
-        for g in range(PASSES):
-            for j in range(PACK * g, PACK * (g + 1)):
-                square = psum.tile([P, BANK], F32, tag="bank", name="square")
-                for i in range(TOKEN_TILES):
-                    nc.tensor.transpose(
-                        square[:, P * i : P * (i + 1)], normed[i][:, P * j : P * (j + 1)], identity[:]
-                    )
-                nc.scalar.activation(
-                    out=h_rows[:, j, :],
-                    in_=square[:],
-                    func=ACT.Identity,
-                    scale=gain_cols[:, j : j + 1],
-                    bias=gain_cols[:, D_SQUARES + j : D_SQUARES + j + 1],
-                )
-            h_grouped = regroup(h_stage, nc.vector.tensor_copy, h_rows[:, PACK * g : PACK * (g + 1), :])
-            quantise_piece(g)
-            quantise(h_grouped, h_codes[:, g, :], h_scales[:, g, :])
+                normalise(i - 1, nc.gpsimd)
+            take_stats(i, range(2, CHUNKS))
+        quantise_piece(0)
+        aggregate(TOKEN_TILES - 1)
+        quantise_piece(1)
+        take_rstd(TOKEN_TILES - 1)
+        gain_cols = keep.tile([P, 2 * D_SQUARES], F32, name="gain_cols")
+        nc.gpsimd.tensor_copy(out=gain_cols[:], in_=gain_raw[:].rearrange("p s g t -> p (s g t)"))
+        normalise(2, nc.vector)
+        normalise(3, nc.vector)
+        regroup_piece_via_tensor(5)
+        regroup_piece(6, nc.vector.tensor_copy)
+        quantise_piece(2)
 
         block_sums = {}
 
@@ -215,8 +213,9 @@ def tile_transformerlayer_pa_kernel(
             b, g = divmod(u, PASSES)
             width = piece_rows[u].shape[2]
             if g == 0:
+                pool = shared_banks if b % 2 else even_sums
                 block_sums[b] = [
-                    psum.tile([P, BANK], F32, tag="bank", name="sums%d" % i) for i in range(TOKEN_TILES)
+                    pool.tile([P, BANK], F32, tag="bank", name="bank") for i in range(TOKEN_TILES)
                 ]
             for i in range(TOKEN_TILES):
                 nc.tensor.matmul_mx(
@@ -245,14 +244,53 @@ def tile_transformerlayer_pa_kernel(
                     nc.sync.dma_start(out=k_tiles[i], in_=result[:, 0:HEAD])
                     nc.sync.dma_start(out=v_tiles[i], in_=result[:, HEAD : 2 * HEAD])
 
-        for u in range(PIECES):
+        h_rows = keep.tile([P, D_SQUARES, TOKENS], BF16, name="h_rows")
+        h_codes = keep.tile([P, PASSES, TOKENS], U32, name="h_codes", align_bytes=64)
+        h_scales = keep.tile([P, PASSES, TOKENS], U8, name="h_scales", align_bytes=64)
+
+        def transpose_pass(g):
+            for j in range(PACK * g, PACK * (g + 1)):
+                square = shared_banks.tile([P, BANK], F32, tag="bank", name="bank")
+                for i in range(TOKEN_TILES):
+                    nc.tensor.transpose(
+                        square[:, P * i : P * (i + 1)], normed[i][:, P * j : P * (j + 1)], identity[:]
+                    )
+                nc.scalar.activation(
+                    out=h_rows[:, j, :],
+                    in_=square[:],
+                    func=ACT.Identity,
+                    scale=gain_cols[:, j : j + 1],
+                    bias=gain_cols[:, D_SQUARES + j : D_SQUARES + j + 1],
+                )
+
+        def regroup_pass(g):
+            return regroup(h_stage, nc.vector.tensor_copy, h_rows[:, PACK * g : PACK * (g + 1), :])
+
+        def quantise_pass(g, h_grouped):
+            quantise(h_grouped, h_codes[:, g, :], h_scales[:, g, :])
+
+        transpose_pass(0)
+        transpose_pass(1)
+        transpose_pass(2)
+        for g in range(PASSES):
+            h_grouped = regroup_pass(g)
+            quantise_piece(g + 3)
+            quantise_pass(g, h_grouped)
+            multiply_piece(g)
+            if g == 0:
+                transpose_pass(3)
+            else:
+                regroup_piece_via_tensor(g + 6)
+        regroup_piece(10, nc.scalar.copy)
+
+        for u in range(PASSES, PIECES):
             b, g = divmod(u, PASSES)
             ahead = u + AHEAD
-            if EARLY_PIECES <= ahead < PIECES:
-                regroup_piece(ahead, nc.vector.tensor_copy if ahead % PASSES == 0 else nc.scalar.copy)
-            if u >= EARLY_PIECES:
+            if 10 < ahead < PIECES:
+                regroup_piece(ahead, nc.vector.tensor_copy if ahead == 11 else nc.scalar.copy)
+            if u > 6:
                 quantise_piece(u)
             multiply_piece(u)
-            if g == 2 and b > 0:
+            if g == 1:
                 finish_block(b - 1)
         finish_block(BLOCKS - 1)

@@ -23,7 +23,6 @@ TOKEN_TILES = TOKENS // P
 D_SQUARES = D // P
 PASSES = D // (P * PACK)
 BANK = 512
-BF16_BANK = 2 * BANK
 STATS_CHUNK = 512
 CHUNKS = D // STATS_CHUNK
 RUN = 4
@@ -31,9 +30,8 @@ RUN = 4
 Q_BLOCKS = Q_COLS // BANK
 BLOCKS = Q_BLOCKS + 1
 PIECES = BLOCKS * PASSES
-AHEAD = 3
 GROUPED_BUFS = 8
-LOADED_BUFS = 16
+LOADED_BUFS = 14
 BIAS_AFTER_PIECE = 11
 
 FLOPS = 2 * TOKENS * D * (Q_COLS + 2 * HEAD)
@@ -58,9 +56,10 @@ def tile_transformerlayer_pa_kernel(
         small = ctx.enter_context(tc.tile_pool(name="small", bufs=TOKEN_TILES))
         loaded = ctx.enter_context(tc.tile_pool(name="loaded", bufs=LOADED_BUFS))
         stage = ctx.enter_context(tc.tile_pool(name="stage", bufs=GROUPED_BUFS))
+        lone_stage = ctx.enter_context(tc.tile_pool(name="lone_stage", bufs=1))
         h_stage = ctx.enter_context(tc.tile_pool(name="h_stage", bufs=2))
         quantised = ctx.enter_context(tc.tile_pool(name="quantised", bufs=3))
-        results = ctx.enter_context(tc.tile_pool(name="results", bufs=6))
+        results = ctx.enter_context(tc.tile_pool(name="results", bufs=8))
         even_sums = ctx.enter_context(tc.psum_pool(name="even_sums", bufs=TOKEN_TILES))
         shared_banks = ctx.enter_context(tc.psum_pool(name="shared_banks", bufs=TOKEN_TILES))
 
@@ -70,8 +69,6 @@ def tile_transformerlayer_pa_kernel(
         nc.scalar.activation(out=warm[:], in_=minus_half[:], func=ACT.Identity)
         identity = keep.tile([P, P], F32, name="identity")
         make_identity(nc, identity[:])
-        identity_bf16 = keep.tile([P, P], BF16, name="identity_bf16")
-        nc.vector.tensor_copy(out=identity_bf16[:], in_=identity[:])
 
         piece_rows = []
 
@@ -122,25 +119,10 @@ def tile_transformerlayer_pa_kernel(
         block_scales = {}
 
         def regroup_piece(u, copy):
-            piece_grouped[u] = regroup(stage, copy, piece_rows[u])
+            piece_grouped[u] = regroup(lone_stage if u % PASSES == 1 and u > PASSES else stage, copy, piece_rows[u])
 
-        def regroup_piece_via_tensor(u):
-            grouped = stage.tile([P, BANK, PACK], BF16, align_bytes=64, name="grouped")
-            flat = grouped[:].rearrange("p w t -> p (w t)")
-            columns = BANK // PACK
-            for half in range(2):
-                bank = shared_banks.tile([P, BF16_BANK], BF16, tag="bank", name="bank")
-                for c in range(2):
-                    first = columns * (2 * half + c)
-                    nc.tensor.matmul(
-                        out=bank[:, BANK * c : BANK * (c + 1)].rearrange("p (w t) -> p w t", t=PACK),
-                        lhsT=identity_bf16[:],
-                        rhs=piece_rows[u][:, :, first : first + columns].rearrange("p t w -> p w t"),
-                        start=True,
-                        stop=True,
-                    )
-                nc.scalar.copy(out=flat[:, BF16_BANK * half : BF16_BANK * (half + 1)], in_=bank[:])
-            piece_grouped[u] = flat
+        def gpsimd_copy(out, in_):
+            nc.gpsimd.tensor_scalar(out=out, in0=in_, scalar1=1.0, scalar2=0.0, op0=ALU.mult, op1=ALU.add)
 
         def quantise_piece(u):
             b, g = divmod(u, PASSES)
@@ -171,41 +153,50 @@ def tile_transformerlayer_pa_kernel(
             nc.vector.tensor_scalar_mul(out=minus_mean[i][:], in0=mean_var[i][:, 0:1], scalar1=-1.0)
             nc.gpsimd.tensor_tensor(out=rstd[i][:], in0=var_eps[:], in1=minus_half[:], op=ALU.pow)
 
-        def normalise(i, engine):
-            engine.tensor_scalar(
+        def normalise_on_scalar(i):
+            shift = small.tile([P, 1], F32, name="shift")
+            nc.gpsimd.tensor_tensor(out=shift[:], in0=minus_mean[i][:], in1=rstd[i][:], op=ALU.mult)
+            nc.scalar.activation(
                 out=normed[i][:].rearrange("p (g t q) -> p g t q", q=P, t=PACK),
-                in0=x_sb[i][:].rearrange("p (g q t) -> p g t q", q=P, t=PACK),
+                in_=x_sb[i][:].rearrange("p (g q t) -> p g t q", q=P, t=PACK),
+                func=ACT.Identity,
+                scale=rstd[i][:],
+                bias=shift[:],
+            )
+
+        def normalise(i, engine, passes=slice(0, PASSES)):
+            engine.tensor_scalar(
+                out=normed[i][:].rearrange("p (g t q) -> p g t q", q=P, t=PACK)[:, passes],
+                in0=x_sb[i][:].rearrange("p (g q t) -> p g t q", q=P, t=PACK)[:, passes],
                 scalar1=minus_mean[i][:],
                 scalar2=rstd[i][:],
                 op0=ALU.add,
                 op1=ALU.mult,
             )
 
+        gain_cols = keep.tile([P, 2 * D_SQUARES], F32, name="gain_cols")
         take_stats(0, range(CHUNKS))
         regroup_piece(0, nc.scalar.copy)
         regroup_piece(1, nc.scalar.copy)
-        regroup_piece_via_tensor(2)
-        regroup_piece_via_tensor(3)
-        regroup_piece_via_tensor(4)
+        regroup_piece(2, nc.scalar.copy)
         for i in range(1, TOKEN_TILES):
             take_stats(i, range(1))
             aggregate(i - 1)
             take_stats(i, range(1, 2))
             take_rstd(i - 1)
-            if i < TOKEN_TILES - 1:
-                normalise(i - 1, nc.gpsimd)
+            if i == 1:
+                normalise(0, nc.gpsimd)
+            if i == 2:
+                normalise_on_scalar(1)
             take_stats(i, range(2, CHUNKS))
-        quantise_piece(0)
-        aggregate(TOKEN_TILES - 1)
-        quantise_piece(1)
-        take_rstd(TOKEN_TILES - 1)
-        gain_cols = keep.tile([P, 2 * D_SQUARES], F32, name="gain_cols")
+        normalise(2, nc.vector, slice(0, 2))
+        aggregate(3)
+        normalise(2, nc.vector, slice(2, 4))
+        take_rstd(3)
         nc.gpsimd.tensor_copy(out=gain_cols[:], in_=gain_raw[:].rearrange("p s g t -> p (s g t)"))
-        normalise(2, nc.vector)
         normalise(3, nc.vector)
-        regroup_piece_via_tensor(5)
-        regroup_piece(6, nc.vector.tensor_copy)
-        quantise_piece(2)
+        quantise_piece(0)
+        regroup_piece(3, nc.scalar.copy)
 
         block_sums = {}
 
@@ -269,28 +260,32 @@ def tile_transformerlayer_pa_kernel(
         def quantise_pass(g, h_grouped):
             quantise(h_grouped, h_codes[:, g, :], h_scales[:, g, :])
 
-        transpose_pass(0)
-        transpose_pass(1)
-        transpose_pass(2)
+        for g in range(PASSES - 1):
+            transpose_pass(g)
+        regroup_piece(4, nc.vector.tensor_copy)
+        quantise_piece(1)
+        quantise_piece(2)
         for g in range(PASSES):
             h_grouped = regroup_pass(g)
-            quantise_piece(g + 3)
+            if g < 2:
+                quantise_piece(g + 3)
+            else:
+                regroup_piece(g + 3, nc.vector.tensor_copy)
             quantise_pass(g, h_grouped)
             multiply_piece(g)
             if g == 0:
                 transpose_pass(3)
-            else:
-                regroup_piece_via_tensor(g + 6)
-        regroup_piece(10, nc.scalar.copy)
+        regroup_piece(7, nc.scalar.copy)
+        regroup_piece(8, nc.scalar.copy)
 
         for u in range(PASSES, PIECES):
             b, g = divmod(u, PASSES)
-            ahead = u + AHEAD
-            if 10 < ahead < PIECES:
-                regroup_piece(ahead, nc.vector.tensor_copy if ahead == 11 else nc.scalar.copy)
-            if u > 6:
+            if u > 4:
                 quantise_piece(u)
+            ahead = u + 4
+            if 8 < ahead < PIECES:
+                regroup_piece(ahead, gpsimd_copy if g == 1 else nc.scalar.copy)
             multiply_piece(u)
-            if g == 1:
+            if g == (3 if b == BLOCKS - 1 else 1):
                 finish_block(b - 1)
         finish_block(BLOCKS - 1)

@@ -23,6 +23,7 @@ TOKEN_TILES = TOKENS // P
 D_SQUARES = D // P
 PASSES = D // (P * PACK)
 BANK = 512
+BF16_BANK = 2 * BANK
 STATS_CHUNK = 512
 CHUNKS = D // STATS_CHUNK
 RUN = 4
@@ -69,6 +70,8 @@ def tile_transformerlayer_pa_kernel(
         nc.scalar.activation(out=warm[:], in_=minus_half[:], func=ACT.Identity)
         identity = keep.tile([P, P], F32, name="identity")
         make_identity(nc, identity[:])
+        identity_bf16 = keep.tile([P, P], BF16, name="identity_bf16")
+        nc.vector.tensor_copy(out=identity_bf16[:], in_=identity[:])
 
         piece_rows = []
 
@@ -119,10 +122,28 @@ def tile_transformerlayer_pa_kernel(
         block_scales = {}
 
         def regroup_piece(u, copy):
-            piece_grouped[u] = regroup(lone_stage if u % PASSES == 1 and u > PASSES else stage, copy, piece_rows[u])
+            piece_grouped[u] = regroup(lone_stage if u == 7 or u in (9, 13, 17) else stage, copy, piece_rows[u])
 
         def gpsimd_copy(out, in_):
             nc.gpsimd.tensor_scalar(out=out, in0=in_, scalar1=1.0, scalar2=0.0, op0=ALU.mult, op1=ALU.add)
+
+        def regroup_piece_via_tensor(u, copy):
+            grouped = stage.tile([P, BANK, PACK], BF16, align_bytes=64, name="grouped")
+            flat = grouped[:].rearrange("p w t -> p (w t)")
+            columns = BANK // PACK
+            for half in range(2):
+                bank = shared_banks.tile([P, BF16_BANK], BF16, tag="bank", name="bank")
+                for c in range(2):
+                    first = columns * (2 * half + c)
+                    nc.tensor.matmul(
+                        out=bank[:, BANK * c : BANK * (c + 1)].rearrange("p (w t) -> p t w", t=PACK),
+                        lhsT=identity_bf16[:],
+                        rhs=piece_rows[u][:, :, first : first + columns],
+                        start=True,
+                        stop=True,
+                    )
+                copy(out=flat[:, BF16_BANK * half : BF16_BANK * (half + 1)], in_=bank[:])
+            piece_grouped[u] = flat
 
         def quantise_piece(u):
             b, g = divmod(u, PASSES)
@@ -178,7 +199,7 @@ def tile_transformerlayer_pa_kernel(
         take_stats(0, range(CHUNKS))
         regroup_piece(0, nc.scalar.copy)
         regroup_piece(1, nc.scalar.copy)
-        regroup_piece(2, nc.scalar.copy)
+        regroup_piece_via_tensor(2, nc.scalar.copy)
         for i in range(1, TOKEN_TILES):
             take_stats(i, range(1))
             aggregate(i - 1)
@@ -196,7 +217,8 @@ def tile_transformerlayer_pa_kernel(
         nc.gpsimd.tensor_copy(out=gain_cols[:], in_=gain_raw[:].rearrange("p s g t -> p (s g t)"))
         normalise(3, nc.vector)
         quantise_piece(0)
-        regroup_piece(3, nc.scalar.copy)
+        regroup_piece_via_tensor(3, nc.scalar.copy)
+        regroup_piece_via_tensor(4, nc.scalar.copy)
 
         block_sums = {}
 
@@ -260,32 +282,31 @@ def tile_transformerlayer_pa_kernel(
         def quantise_pass(g, h_grouped):
             quantise(h_grouped, h_codes[:, g, :], h_scales[:, g, :])
 
-        for g in range(PASSES - 1):
-            transpose_pass(g)
-        regroup_piece(4, nc.vector.tensor_copy)
+        transpose_pass(0)
+        regroup_piece_via_tensor(5, nc.scalar.copy)
+        transpose_pass(1)
+        transpose_pass(2)
         quantise_piece(1)
+        regroup_piece(6, nc.vector.tensor_copy)
         quantise_piece(2)
+        regroup_piece(7, nc.vector.tensor_copy)
         for g in range(PASSES):
             h_grouped = regroup_pass(g)
-            if g < 2:
-                quantise_piece(g + 3)
-            else:
-                regroup_piece(g + 3, nc.vector.tensor_copy)
+            quantise_piece(g + 3)
             quantise_pass(g, h_grouped)
             multiply_piece(g)
             if g == 0:
                 transpose_pass(3)
-        regroup_piece(7, nc.scalar.copy)
         regroup_piece(8, nc.scalar.copy)
 
         for u in range(PASSES, PIECES):
             b, g = divmod(u, PASSES)
-            if u > 4:
+            if u > 6:
                 quantise_piece(u)
             ahead = u + 4
             if 8 < ahead < PIECES:
-                regroup_piece(ahead, gpsimd_copy if g == 1 else nc.scalar.copy)
+                regroup_piece(ahead, gpsimd_copy if ahead in (9, 13, 17) else (nc.vector.tensor_copy if ahead in (18,) else nc.scalar.copy))
             multiply_piece(u)
-            if g == (3 if b == BLOCKS - 1 else 1):
+            if u in (7, 9, 13, 19):
                 finish_block(b - 1)
         finish_block(BLOCKS - 1)

@@ -105,13 +105,19 @@ def tile_transformerlayer_pa_kernel(
                 nc.sync.dma_start(out=bias_all[:, Q_COLS : Q_COLS + HEAD], in_=wk_b.partition_broadcast(P))
                 nc.sync.dma_start(out=bias_all[:, Q_COLS + HEAD :], in_=wv_b.partition_broadcast(P))
 
+        def gpsimd_copy(out, in_):
+            nc.gpsimd.tensor_scalar(out=out, in0=in_, scalar1=1.0, scalar2=0.0, op0=ALU.mult, op1=ALU.add)
+
         def regroup(pool, copy, rows):
             width = rows.shape[2]
             grouped = pool.tile([P, BANK, PACK], BF16, align_bytes=64, name="grouped")
-            copy(
-                out=grouped[:, :width, :].rearrange("p (c i) t -> p c t i", i=RUN),
-                in_=rows.rearrange("p t (c i) -> p c t i", i=RUN),
-            )
+            if copy == gpsimd_copy:
+                copy(out=grouped[:, :width, :], in_=rows.rearrange("p t c -> p c t"))
+            else:
+                copy(
+                    out=grouped[:, :width, :].rearrange("p (c i) t -> p c t i", i=RUN),
+                    in_=rows.rearrange("p t (c i) -> p c t i", i=RUN),
+                )
             return grouped[:, :width, :].rearrange("p w t -> p (w t)")
 
         def quantise(grouped, codes, scales):
@@ -124,8 +130,6 @@ def tile_transformerlayer_pa_kernel(
         def regroup_piece(u, copy):
             piece_grouped[u] = regroup(lone_stage if u == 7 or u in (9, 13, 17) else stage, copy, piece_rows[u])
 
-        def gpsimd_copy(out, in_):
-            nc.gpsimd.tensor_scalar(out=out, in0=in_, scalar1=1.0, scalar2=0.0, op0=ALU.mult, op1=ALU.add)
 
         def regroup_piece_via_tensor(u, copy):
             grouped = stage.tile([P, BANK, PACK], BF16, align_bytes=64, name="grouped")

@@ -23,10 +23,9 @@ TOKEN_TILES = TOKENS // P
 D_SQUARES = D // P
 PASSES = D // (P * PACK)
 BANK = 512
-BF16_BANK = 2 * BANK
 STATS_CHUNK = 512
 CHUNKS = D // STATS_CHUNK
-RUN = 4
+RUN = 2
 
 Q_BLOCKS = Q_COLS // BANK
 BLOCKS = Q_BLOCKS + 1
@@ -70,8 +69,6 @@ def tile_transformerlayer_pa_kernel(
         nc.scalar.activation(out=warm[:], in_=minus_half[:], func=ACT.Identity)
         identity = keep.tile([P, P], F32, name="identity")
         make_identity(nc, identity[:])
-        identity_bf16 = keep.tile([P, P], BF16, name="identity_bf16")
-        nc.vector.tensor_copy(out=identity_bf16[:], in_=identity[:])
 
         piece_rows = []
 
@@ -131,24 +128,6 @@ def tile_transformerlayer_pa_kernel(
             piece_grouped[u] = regroup(lone_stage if u == 7 or u in (9, 13, 17) else stage, copy, piece_rows[u])
 
 
-        def regroup_piece_via_tensor(u, copy):
-            grouped = stage.tile([P, BANK, PACK], BF16, align_bytes=64, name="grouped")
-            flat = grouped[:].rearrange("p w t -> p (w t)")
-            columns = BANK // PACK
-            for half in range(2):
-                bank = shared_banks.tile([P, BF16_BANK], BF16, tag="bank", name="bank")
-                for c in range(2):
-                    first = columns * (2 * half + c)
-                    nc.tensor.matmul(
-                        out=bank[:, BANK * c : BANK * (c + 1)].rearrange("p (w t) -> p t w", t=PACK),
-                        lhsT=identity_bf16[:],
-                        rhs=piece_rows[u][:, :, first : first + columns],
-                        start=True,
-                        stop=True,
-                    )
-                copy(out=flat[:, BF16_BANK * half : BF16_BANK * (half + 1)], in_=bank[:])
-            piece_grouped[u] = flat
-
         def quantise_piece(u):
             b, g = divmod(u, PASSES)
             if g == 0:
@@ -203,7 +182,7 @@ def tile_transformerlayer_pa_kernel(
         take_stats(0, range(CHUNKS))
         regroup_piece(0, nc.scalar.copy)
         regroup_piece(1, nc.scalar.copy)
-        regroup_piece_via_tensor(2, nc.scalar.copy)
+        regroup_piece(2, nc.scalar.copy)
         for i in range(1, TOKEN_TILES):
             take_stats(i, range(1))
             aggregate(i - 1)
@@ -221,8 +200,7 @@ def tile_transformerlayer_pa_kernel(
         nc.gpsimd.tensor_copy(out=gain_cols[:], in_=gain_raw[:].rearrange("p s g t -> p (s g t)"))
         normalise(3, nc.vector)
         quantise_piece(0)
-        regroup_piece_via_tensor(3, nc.scalar.copy)
-        regroup_piece_via_tensor(4, nc.scalar.copy)
+        regroup_piece(3, nc.scalar.copy)
 
         block_sums = {}
 
@@ -287,25 +265,28 @@ def tile_transformerlayer_pa_kernel(
             quantise(h_grouped, h_codes[:, g, :], h_scales[:, g, :])
 
         transpose_pass(0)
-        regroup_piece_via_tensor(5, nc.scalar.copy)
         transpose_pass(1)
         transpose_pass(2)
         quantise_piece(1)
-        regroup_piece(6, nc.vector.tensor_copy)
+        regroup_piece(4, nc.vector.tensor_copy)
         quantise_piece(2)
-        regroup_piece(7, nc.vector.tensor_copy)
+        regroup_piece(5, nc.vector.tensor_copy)
         for g in range(PASSES):
             h_grouped = regroup_pass(g)
-            quantise_piece(g + 3)
+            if g < 3:
+                quantise_piece(g + 3)
+            else:
+                regroup_piece(7, nc.vector.tensor_copy)
             quantise_pass(g, h_grouped)
             multiply_piece(g)
             if g == 0:
                 transpose_pass(3)
+        regroup_piece(6, nc.scalar.copy)
         regroup_piece(8, nc.scalar.copy)
 
         for u in range(PASSES, PIECES):
             b, g = divmod(u, PASSES)
-            if u > 6:
+            if u > 5:
                 quantise_piece(u)
             ahead = u + 4
             if 8 < ahead < PIECES:

@@ -15,14 +15,18 @@ P = 128
 PACK = 4
 TOKENS = 512
 D = 2048
-Q_COLS = 2048
 HEAD = 128
+Q_HEADS = 16
+HEADS = Q_HEADS + 2
+Q_COLS = Q_HEADS * HEAD
 EPS = 1e-05
 
 TOKEN_TILES = TOKENS // P
 D_SQUARES = D // P
-PASSES = D // (P * PACK)
+PASS_D = P * PACK
+PASSES = D // PASS_D
 BANK = 512
+BF16_BANK = 2 * BANK
 STATS_CHUNK = 512
 CHUNKS = D // STATS_CHUNK
 RUN = 2
@@ -30,9 +34,7 @@ RUN = 2
 Q_BLOCKS = Q_COLS // BANK
 BLOCKS = Q_BLOCKS + 1
 PIECES = BLOCKS * PASSES
-GROUPED_BUFS = 8
-LOADED_BUFS = 14
-BIAS_AFTER_PIECE = 11
+GROUPED_BUFS = 6
 
 FLOPS = 2 * TOKENS * D * (Q_COLS + 2 * HEAD)
 
@@ -44,8 +46,8 @@ def tile_transformerlayer_pa_kernel(
 
     x_tiles = x.rearrange("b (i p) d -> (b i) p d", p=P)
     wq_rows = wq_k.rearrange("(g p t) h e -> g p t (h e)", p=P, t=PACK)
-    wk_rows = wk_k.rearrange("(g p t) e -> g p t e", p=P, t=PACK)
-    wv_rows = wv_k.rearrange("(g p t) e -> g p t e", p=P, t=PACK)
+    wk_rows = wk_k.rearrange("(g p t) e -> p g (t e)", p=P, t=PACK)
+    wv_rows = wv_k.rearrange("(g p t) e -> p g (t e)", p=P, t=PACK)
     q_tiles = out_0.rearrange("b (i p) h e -> (b i) p (h e)", p=P)
     k_tiles = out_1.rearrange("b (i p) e -> (b i) p e", p=P)
     v_tiles = out_2.rearrange("b (i p) e -> (b i) p e", p=P)
@@ -54,7 +56,7 @@ def tile_transformerlayer_pa_kernel(
         ctx.enter_context(tc.manual_schedule())
         keep = ctx.enter_context(tc.tile_pool(name="keep", bufs=1))
         small = ctx.enter_context(tc.tile_pool(name="small", bufs=TOKEN_TILES))
-        loaded = ctx.enter_context(tc.tile_pool(name="loaded", bufs=LOADED_BUFS))
+        loaded = ctx.enter_context(tc.tile_pool(name="loaded", bufs=1))
         stage = ctx.enter_context(tc.tile_pool(name="stage", bufs=GROUPED_BUFS))
         lone_stage = ctx.enter_context(tc.tile_pool(name="lone_stage", bufs=1))
         h_stage = ctx.enter_context(tc.tile_pool(name="h_stage", bufs=2))
@@ -67,40 +69,68 @@ def tile_transformerlayer_pa_kernel(
         nc.vector.memset(minus_half[:], -0.5)
         warm = keep.tile([P, 1], F32, name="warm")
         nc.scalar.activation(out=warm[:], in_=minus_half[:], func=ACT.Identity)
+        small_rows = keep.tile([P, PASS_D + HEAD], BF16, name="small_rows")
+        nc.vector.memset(small_rows[:], 0.0)
+        nc.scalar.dma_start(
+            out=small_rows[0:PASSES, 0:PASS_D], in_=ln1_s.rearrange("(g d) -> g d", d=PASS_D)
+        )
+        nc.scalar.dma_start(
+            out=small_rows[PASSES : 2 * PASSES, 0:PASS_D], in_=ln1_b.rearrange("(g d) -> g d", d=PASS_D)
+        )
+        nc.scalar.dma_start(out=small_rows[0:Q_HEADS, PASS_D:], in_=wq_b)
+        nc.scalar.dma_start(
+            out=small_rows[Q_HEADS : Q_HEADS + 1, PASS_D:], in_=wk_b.rearrange("(a e) -> a e", a=1)
+        )
+        nc.scalar.dma_start(
+            out=small_rows[Q_HEADS + 1 : Q_HEADS + 2, PASS_D:], in_=wv_b.rearrange("(a e) -> a e", a=1)
+        )
         identity = keep.tile([P, P], F32, name="identity")
         make_identity(nc, identity[:])
+        identity_bf16 = keep.tile([P, P], BF16, name="identity_bf16")
+        nc.vector.tensor_copy(out=identity_bf16[:], in_=identity[:])
 
-        piece_rows = []
+        gain_bank = shared_banks.tile([P, PACK, P], BF16, tag="bank", name="bank")
+        for t in range(PACK):
+            nc.tensor.transpose(gain_bank[:, t, :], small_rows[:, t:PASS_D:PACK], identity_bf16[:])
+        gain_cols = keep.tile([P, 2 * PASSES, PACK], F32, name="gain_cols")
 
-        def load_piece():
-            b, g = divmod(len(piece_rows), PASSES)
-            rows = loaded.tile([P, PACK, BANK], BF16, name="rows")
-            if b < Q_BLOCKS:
-                nc.sync.dma_start(out=rows[:], in_=wq_rows[g][:, :, BANK * b : BANK * (b + 1)])
-                piece_rows.append(rows[:])
-            else:
-                nc.sync.dma_start(out=rows[:, :, 0:HEAD], in_=wk_rows[g])
-                nc.sync.dma_start(out=rows[:, :, HEAD : 2 * HEAD], in_=wv_rows[g])
-                piece_rows.append(rows[:, :, 0 : 2 * HEAD])
+        heads_a_bank = BF16_BANK // HEAD
+        bias_banks = []
+        for first in range(0, HEADS, heads_a_bank):
+            bias_bank = shared_banks.tile([P, BF16_BANK], BF16, tag="bank", name="bank")
+            bias_banks.append(bias_bank)
+            for r in range(first, min(first + heads_a_bank, HEADS)):
+                nc.tensor.matmul(
+                    out=bias_bank[:, HEAD * (r - first) : HEAD * (r - first + 1)],
+                    lhsT=identity_bf16[:, r : r + 1].to_broadcast([P, P]),
+                    rhs=small_rows[:, PASS_D:],
+                    start=True,
+                    stop=True,
+                )
+        bias_all = keep.tile([P, HEAD * HEADS], BF16, name="bias_all")
+
+        piece_rows = {}
+
+        def load_pieces(blocks, g):
+            first, last = BANK * blocks[0], BANK * (blocks[-1] + 1)
+            rows = loaded.tile([P, PACK, last - first], BF16, name="rows%d_%d" % (blocks[0], g))
+            nc.sync.dma_start(out=rows[:], in_=wq_rows[g][:, :, first:last])
+            for b in blocks:
+                piece_rows[PASSES * b + g] = rows[:, :, BANK * b - first : BANK * (b + 1) - first]
 
         x_sb = []
         for i in range(TOKEN_TILES):
             x_i = keep.tile([P, D], BF16, name="x%d" % i)
             nc.sync.dma_start(out=x_i[:], in_=x_tiles[i])
             x_sb.append(x_i)
-            load_piece()
-        gain_raw = keep.tile([P, 2, PASSES, PACK], BF16, name="gain_raw")
-        nc.sync.dma_start(out=gain_raw[:, 0, :, :], in_=ln1_s.rearrange("(g p t) -> p g t", p=P, t=PACK))
-        nc.sync.dma_start(out=gain_raw[:, 1, :, :], in_=ln1_b.rearrange("(g p t) -> p g t", p=P, t=PACK))
-        bias_all = keep.tile([P, Q_COLS + 2 * HEAD], BF16, name="bias_all")
-        for u in range(TOKEN_TILES, PIECES):
-            load_piece()
-            if u == BIAS_AFTER_PIECE:
-                nc.sync.dma_start(
-                    out=bias_all[:, 0:Q_COLS], in_=wq_b.rearrange("h e -> (h e)").partition_broadcast(P)
-                )
-                nc.sync.dma_start(out=bias_all[:, Q_COLS : Q_COLS + HEAD], in_=wk_b.partition_broadcast(P))
-                nc.sync.dma_start(out=bias_all[:, Q_COLS + HEAD :], in_=wv_b.partition_broadcast(P))
+            load_pieces([0], i)
+        for g in range(PASSES):
+            load_pieces([1], g)
+        for g in range(PASSES):
+            load_pieces([2, 3], g)
+        kv_rows = loaded.tile([P, 2, PASSES, PACK, HEAD], BF16, name="kv_rows")
+        nc.sync.dma_start(out=kv_rows[:, 0].rearrange("p g t e -> p g (t e)"), in_=wk_rows)
+        nc.sync.dma_start(out=kv_rows[:, 1].rearrange("p g t e -> p g (t e)"), in_=wv_rows)
 
         def gpsimd_copy(out, in_):
             nc.gpsimd.tensor_scalar(out=out, in0=in_, scalar1=1.0, scalar2=0.0, op0=ALU.mult, op1=ALU.add)
@@ -120,20 +150,32 @@ def tile_transformerlayer_pa_kernel(
         def quantise(grouped, codes, scales):
             nc.vector.quantize_mx(out=codes.bitcast(FP8X4), scales=scales, in_=grouped)
 
+        def block_width(b):
+            return BANK if b < Q_BLOCKS else 2 * HEAD
+
         piece_grouped = {}
         block_codes = {}
         block_scales = {}
 
         def regroup_piece(u, copy):
-            piece_grouped[u] = regroup(lone_stage if u == 7 or u in (9, 13, 17) else stage, copy, piece_rows[u])
-
+            b, g = divmod(u, PASSES)
+            pool = lone_stage if u == 7 or u in (9, 13, 17) else stage
+            if b < Q_BLOCKS:
+                piece_grouped[u] = regroup(pool, copy, piece_rows[u])
+            else:
+                grouped = pool.tile([P, BANK, PACK], BF16, align_bytes=64, name="grouped")
+                copy(
+                    out=grouped[:, 0 : 2 * HEAD, :].rearrange("p (k e) t -> p k e t", k=2),
+                    in_=kv_rows[:, :, g].rearrange("p k t e -> p k e t"),
+                )
+                piece_grouped[u] = grouped[:, 0 : 2 * HEAD, :].rearrange("p w t -> p (w t)")
 
         def quantise_piece(u):
             b, g = divmod(u, PASSES)
+            width = block_width(b)
             if g == 0:
                 block_codes[b] = quantised.tile([P, PASSES, BANK], U32, name="w_codes", align_bytes=64)
                 block_scales[b] = quantised.tile([P, PASSES, BANK], U8, name="w_scales", align_bytes=64)
-            width = piece_rows[u].shape[2]
             quantise(piece_grouped[u], block_codes[b][:, g, :width], block_scales[b][:, g, :width])
 
         stats = [small.tile([P, CHUNKS, 6], F32, name="stats") for i in range(TOKEN_TILES)]
@@ -178,7 +220,6 @@ def tile_transformerlayer_pa_kernel(
                 op1=ALU.mult,
             )
 
-        gain_cols = keep.tile([P, 2 * D_SQUARES], F32, name="gain_cols")
         take_stats(0, range(CHUNKS))
         regroup_piece(0, nc.scalar.copy)
         regroup_piece(1, nc.scalar.copy)
@@ -197,7 +238,14 @@ def tile_transformerlayer_pa_kernel(
         aggregate(3)
         normalise(2, nc.vector, slice(2, 4))
         take_rstd(3)
-        nc.gpsimd.tensor_copy(out=gain_cols[:], in_=gain_raw[:].rearrange("p s g t -> p (s g t)"))
+        nc.vector.tensor_copy(
+            out=gain_cols[:], in_=gain_bank[:, :, 0 : 2 * PASSES].rearrange("p t r -> p r t")
+        )
+        for c in range(len(bias_banks)):
+            columns = min(BF16_BANK, HEAD * HEADS - BF16_BANK * c)
+            nc.vector.tensor_copy(
+                out=bias_all[:, BF16_BANK * c : BF16_BANK * c + columns], in_=bias_banks[c][:, :columns]
+            )
         normalise(3, nc.vector)
         quantise_piece(0)
         regroup_piece(3, nc.scalar.copy)
@@ -206,7 +254,7 @@ def tile_transformerlayer_pa_kernel(
 
         def multiply_piece(u):
             b, g = divmod(u, PASSES)
-            width = piece_rows[u].shape[2]
+            width = block_width(b)
             if g == 0:
                 pool = shared_banks if b % 2 else even_sums
                 block_sums[b] = [
@@ -224,7 +272,7 @@ def tile_transformerlayer_pa_kernel(
                 )
 
         def finish_block(b):
-            width = piece_rows[PASSES * b].shape[2]
+            width = block_width(b)
             for i in range(TOKEN_TILES):
                 result = results.tile([P, BANK], F32, name="result")
                 nc.vector.tensor_tensor(
@@ -243,6 +291,8 @@ def tile_transformerlayer_pa_kernel(
         h_codes = keep.tile([P, PASSES, TOKENS], U32, name="h_codes", align_bytes=64)
         h_scales = keep.tile([P, PASSES, TOKENS], U8, name="h_scales", align_bytes=64)
 
+        gain_flat = gain_cols[:].rearrange("p r t -> p (r t)")
+
         def transpose_pass(g):
             for j in range(PACK * g, PACK * (g + 1)):
                 square = shared_banks.tile([P, BANK], F32, tag="bank", name="bank")
@@ -254,8 +304,8 @@ def tile_transformerlayer_pa_kernel(
                     out=h_rows[:, j, :],
                     in_=square[:],
                     func=ACT.Identity,
-                    scale=gain_cols[:, j : j + 1],
-                    bias=gain_cols[:, D_SQUARES + j : D_SQUARES + j + 1],
+                    scale=gain_flat[:, j : j + 1],
+                    bias=gain_flat[:, D_SQUARES + j : D_SQUARES + j + 1],
                 )
 
         def regroup_pass(g):

@@ -89,24 +89,11 @@ def tile_transformerlayer_pa_kernel(
         identity_bf16 = keep.tile([P, P], BF16, name="identity_bf16")
         nc.vector.tensor_copy(out=identity_bf16[:], in_=identity[:])
 
-        gain_bank = shared_banks.tile([P, PACK, P], BF16, tag="bank", name="bank")
+        gain_bank = even_sums.tile([P, PACK, P], BF16, tag="bank", name="bank")
         for t in range(PACK):
             nc.tensor.transpose(gain_bank[:, t, :], small_rows[:, t:PASS_D:PACK], identity_bf16[:])
         gain_cols = keep.tile([P, 2 * PASSES, PACK], F32, name="gain_cols")
 
-        heads_a_bank = BF16_BANK // HEAD
-        bias_banks = []
-        for first in range(0, HEADS, heads_a_bank):
-            bias_bank = shared_banks.tile([P, BF16_BANK], BF16, tag="bank", name="bank")
-            bias_banks.append(bias_bank)
-            for r in range(first, min(first + heads_a_bank, HEADS)):
-                nc.tensor.matmul(
-                    out=bias_bank[:, HEAD * (r - first) : HEAD * (r - first + 1)],
-                    lhsT=identity_bf16[:, r : r + 1].to_broadcast([P, P]),
-                    rhs=small_rows[:, PASS_D:],
-                    start=True,
-                    stop=True,
-                )
         bias_all = keep.tile([P, HEAD * HEADS], BF16, name="bias_all")
 
         piece_rows = {}
@@ -170,6 +157,24 @@ def tile_transformerlayer_pa_kernel(
                 )
                 piece_grouped[u] = grouped[:, 0 : 2 * HEAD, :].rearrange("p w t -> p (w t)")
 
+        def regroup_piece_via_tensor(u, copy):
+            grouped = stage.tile([P, BANK, PACK], BF16, align_bytes=64, name="grouped")
+            flat = grouped[:].rearrange("p w t -> p (w t)")
+            columns = BANK // PACK
+            for half in range(2):
+                bank = shared_banks.tile([P, BF16_BANK], BF16, tag="bank", name="bank")
+                for c in range(2):
+                    first = columns * (2 * half + c)
+                    nc.tensor.matmul(
+                        out=bank[:, BANK * c : BANK * (c + 1)].rearrange("p (w t) -> p t w", t=PACK),
+                        lhsT=identity_bf16[:],
+                        rhs=piece_rows[u][:, :, first : first + columns],
+                        start=True,
+                        stop=True,
+                    )
+                copy(out=flat[:, BF16_BANK * half : BF16_BANK * (half + 1)], in_=bank[:])
+            piece_grouped[u] = flat
+
         def quantise_piece(u):
             b, g = divmod(u, PASSES)
             width = block_width(b)
@@ -224,6 +229,19 @@ def tile_transformerlayer_pa_kernel(
         regroup_piece(0, nc.scalar.copy)
         regroup_piece(1, nc.scalar.copy)
         regroup_piece(2, nc.scalar.copy)
+        heads_a_bank = BF16_BANK // HEAD
+        bias_banks = []
+        for first in range(0, HEADS, heads_a_bank):
+            bias_bank = even_sums.tile([P, BF16_BANK], BF16, tag="bank", name="bank")
+            bias_banks.append(bias_bank)
+            for r in range(first, min(first + heads_a_bank, HEADS)):
+                nc.tensor.matmul(
+                    out=bias_bank[:, HEAD * (r - first) : HEAD * (r - first + 1)],
+                    lhsT=identity_bf16[:, r : r + 1].to_broadcast([P, P]),
+                    rhs=small_rows[:, PASS_D:],
+                    start=True,
+                    stop=True,
+                )
         for i in range(1, TOKEN_TILES):
             take_stats(i, range(1))
             aggregate(i - 1)
@@ -248,7 +266,8 @@ def tile_transformerlayer_pa_kernel(
             )
         normalise(3, nc.vector)
         quantise_piece(0)
-        regroup_piece(3, nc.scalar.copy)
+        regroup_piece_via_tensor(3, nc.scalar.copy)
+        regroup_piece_via_tensor(4, nc.scalar.copy)
 
         block_sums = {}
 
@@ -315,28 +334,25 @@ def tile_transformerlayer_pa_kernel(
             quantise(h_grouped, h_codes[:, g, :], h_scales[:, g, :])
 
         transpose_pass(0)
+        regroup_piece_via_tensor(5, nc.scalar.copy)
         transpose_pass(1)
         transpose_pass(2)
         quantise_piece(1)
-        regroup_piece(4, nc.vector.tensor_copy)
+        regroup_piece(6, nc.vector.tensor_copy)
         quantise_piece(2)
-        regroup_piece(5, nc.vector.tensor_copy)
+        regroup_piece(7, nc.vector.tensor_copy)
         for g in range(PASSES):
             h_grouped = regroup_pass(g)
-            if g < 3:
-                quantise_piece(g + 3)
-            else:
-                regroup_piece(7, nc.vector.tensor_copy)
+            quantise_piece(g + 3)
             quantise_pass(g, h_grouped)
             multiply_piece(g)
             if g == 0:
                 transpose_pass(3)
-        regroup_piece(6, nc.scalar.copy)
         regroup_piece(8, nc.scalar.copy)
 
         for u in range(PASSES, PIECES):
             b, g = divmod(u, PASSES)
-            if u > 5:
+            if u > 6:
                 quantise_piece(u)
             ahead = u + 4
             if 8 < ahead < PIECES:

@@ -334,20 +334,19 @@ def tile_transformerlayer_pa_kernel(
             quantise(h_grouped, h_codes[:, g, :], h_scales[:, g, :])
 
         transpose_pass(0)
-        regroup_piece_via_tensor(5, nc.scalar.copy)
         transpose_pass(1)
         transpose_pass(2)
+        transpose_pass(3)
         quantise_piece(1)
-        regroup_piece(6, nc.vector.tensor_copy)
+        regroup_piece(5, nc.vector.tensor_copy)
         quantise_piece(2)
-        regroup_piece(7, nc.vector.tensor_copy)
+        regroup_piece(6, nc.vector.tensor_copy)
         for g in range(PASSES):
             h_grouped = regroup_pass(g)
             quantise_piece(g + 3)
             quantise_pass(g, h_grouped)
             multiply_piece(g)
-            if g == 0:
-                transpose_pass(3)
+        regroup_piece(7, nc.scalar.copy)
         regroup_piece(8, nc.scalar.copy)
 
         for u in range(PASSES, PIECES):
@@ -356,8 +355,8 @@ def tile_transformerlayer_pa_kernel(
                 quantise_piece(u)
             ahead = u + 4
             if 8 < ahead < PIECES:
-                regroup_piece(ahead, gpsimd_copy if ahead in (9, 13, 17) else (nc.vector.tensor_copy if ahead in (18,) else nc.scalar.copy))
+                regroup_piece(ahead, gpsimd_copy if ahead in (9, 13, 17) else (nc.vector.tensor_copy if ahead in (10, 18,) else nc.scalar.copy))
             multiply_piece(u)
-            if u in (7, 9, 13, 19):
+            if u in (7, 10, 13, 18):
                 finish_block(b - 1)
         finish_block(BLOCKS - 1)

@@ -18,7 +18,6 @@ D = 2048
 HEAD = 128
 Q_HEADS = 16
 HEADS = Q_HEADS + 2
-Q_COLS = Q_HEADS * HEAD
 EPS = 1e-05
 
 TOKEN_TILES = TOKENS // P
@@ -29,14 +28,15 @@ BANK = 512
 BF16_BANK = 2 * BANK
 STATS_CHUNK = 512
 CHUNKS = D // STATS_CHUNK
-RUN = 2
 
-Q_BLOCKS = Q_COLS // BANK
+Q_BLOCKS = Q_HEADS * HEAD // BANK
 BLOCKS = Q_BLOCKS + 1
 PIECES = BLOCKS * PASSES
+AHEAD = 4
 GROUPED_BUFS = 6
+RUN = {"vector": 2, "scalar": 4, "gpsimd": 1}
 
-FLOPS = 2 * TOKENS * D * (Q_COLS + 2 * HEAD)
+FLOPS = 2 * TOKENS * D * HEADS * HEAD
 
 
 def tile_transformerlayer_pa_kernel(
@@ -62,18 +62,17 @@ def tile_transformerlayer_pa_kernel(
         h_stage = ctx.enter_context(tc.tile_pool(name="h_stage", bufs=2))
         quantised = ctx.enter_context(tc.tile_pool(name="quantised", bufs=3))
         results = ctx.enter_context(tc.tile_pool(name="results", bufs=8))
-        even_sums = ctx.enter_context(tc.psum_pool(name="even_sums", bufs=TOKEN_TILES))
+        even_banks = ctx.enter_context(tc.psum_pool(name="even_banks", bufs=TOKEN_TILES))
         shared_banks = ctx.enter_context(tc.psum_pool(name="shared_banks", bufs=TOKEN_TILES))
 
         minus_half = keep.tile([P, 1], F32, name="minus_half")
         nc.vector.memset(minus_half[:], -0.5)
         warm = keep.tile([P, 1], F32, name="warm")
         nc.scalar.activation(out=warm[:], in_=minus_half[:], func=ACT.Identity)
+
         small_rows = keep.tile([P, PASS_D + HEAD], BF16, name="small_rows")
         nc.vector.memset(small_rows[:], 0.0)
-        nc.scalar.dma_start(
-            out=small_rows[0:PASSES, 0:PASS_D], in_=ln1_s.rearrange("(g d) -> g d", d=PASS_D)
-        )
+        nc.scalar.dma_start(out=small_rows[0:PASSES, 0:PASS_D], in_=ln1_s.rearrange("(g d) -> g d", d=PASS_D))
         nc.scalar.dma_start(
             out=small_rows[PASSES : 2 * PASSES, 0:PASS_D], in_=ln1_b.rearrange("(g d) -> g d", d=PASS_D)
         )
@@ -89,12 +88,23 @@ def tile_transformerlayer_pa_kernel(
         identity_bf16 = keep.tile([P, P], BF16, name="identity_bf16")
         nc.vector.tensor_copy(out=identity_bf16[:], in_=identity[:])
 
-        gain_bank = even_sums.tile([P, PACK, P], BF16, tag="bank", name="bank")
+        gain_bank = even_banks.tile([P, PACK, P], BF16, tag="bank", name="bank")
         for t in range(PACK):
             nc.tensor.transpose(gain_bank[:, t, :], small_rows[:, t:PASS_D:PACK], identity_bf16[:])
-        gain_cols = keep.tile([P, 2 * PASSES, PACK], F32, name="gain_cols")
 
-        bias_all = keep.tile([P, HEAD * HEADS], BF16, name="bias_all")
+        heads_a_bank = BF16_BANK // HEAD
+        bias_banks = []
+        for first in range(0, HEADS, heads_a_bank):
+            bias_bank = even_banks.tile([P, BF16_BANK], BF16, tag="bank", name="bank")
+            bias_banks.append(bias_bank)
+            for r in range(first, min(first + heads_a_bank, HEADS)):
+                nc.tensor.matmul(
+                    out=bias_bank[:, HEAD * (r - first) : HEAD * (r - first + 1)],
+                    lhsT=identity_bf16[:, r : r + 1].to_broadcast([P, P]),
+                    rhs=small_rows[:, PASS_D:],
+                    start=True,
+                    stop=True,
+                )
 
         piece_rows = {}
 
@@ -119,23 +129,27 @@ def tile_transformerlayer_pa_kernel(
         nc.sync.dma_start(out=kv_rows[:, 0].rearrange("p g t e -> p g (t e)"), in_=wk_rows)
         nc.sync.dma_start(out=kv_rows[:, 1].rearrange("p g t e -> p g (t e)"), in_=wv_rows)
 
-        def gpsimd_copy(out, in_):
-            nc.gpsimd.tensor_scalar(out=out, in0=in_, scalar1=1.0, scalar2=0.0, op0=ALU.mult, op1=ALU.add)
-
-        def regroup(pool, copy, rows):
-            width = rows.shape[2]
-            grouped = pool.tile([P, BANK, PACK], BF16, align_bytes=64, name="grouped")
-            if copy == gpsimd_copy:
-                copy(out=grouped[:, :width, :], in_=rows.rearrange("p t c -> p c t"))
+        def copy_on(engine, out, in_):
+            if engine == "vector":
+                nc.vector.tensor_copy(out=out, in_=in_)
+            elif engine == "scalar":
+                nc.scalar.copy(out=out, in_=in_)
             else:
-                copy(
-                    out=grouped[:, :width, :].rearrange("p (c i) t -> p c t i", i=RUN),
-                    in_=rows.rearrange("p t (c i) -> p c t i", i=RUN),
-                )
-            return grouped[:, :width, :].rearrange("p w t -> p (w t)")
+                nc.gpsimd.tensor_scalar(out=out, in0=in_, scalar1=1.0, scalar2=0.0, op0=ALU.mult, op1=ALU.add)
 
-        def quantise(grouped, codes, scales):
-            nc.vector.quantize_mx(out=codes.bitcast(FP8X4), scales=scales, in_=grouped)
+        def regroup(engine, grouped, rows):
+            run = RUN[engine]
+            if run == 1:
+                copy_on(engine, grouped, rows.rearrange("p t c -> p c t"))
+            else:
+                copy_on(
+                    engine,
+                    grouped.rearrange("p (c i) t -> p c t i", i=run),
+                    rows.rearrange("p t (c i) -> p c t i", i=run),
+                )
+
+        def new_group(pool):
+            return pool.tile([P, BANK, PACK], BF16, align_bytes=64, name="grouped")
 
         def block_width(b):
             return BANK if b < Q_BLOCKS else 2 * HEAD
@@ -144,22 +158,26 @@ def tile_transformerlayer_pa_kernel(
         block_codes = {}
         block_scales = {}
 
-        def regroup_piece(u, copy):
+        def regroup_piece(u, engine, pool=stage):
             b, g = divmod(u, PASSES)
-            pool = lone_stage if u == 7 or u in (9, 13, 17) else stage
+            piece_grouped[u] = new_group(pool)
             if b < Q_BLOCKS:
-                piece_grouped[u] = regroup(pool, copy, piece_rows[u])
+                regroup(engine, piece_grouped[u][:], piece_rows[u])
             else:
-                grouped = pool.tile([P, BANK, PACK], BF16, align_bytes=64, name="grouped")
-                copy(
-                    out=grouped[:, 0 : 2 * HEAD, :].rearrange("p (k e) t -> p k e t", k=2),
-                    in_=kv_rows[:, :, g].rearrange("p k t e -> p k e t"),
+                copy_on(
+                    engine,
+                    piece_grouped[u][:, 0 : 2 * HEAD, :].rearrange("p (k e) t -> p k e t", k=2),
+                    kv_rows[:, :, g].rearrange("p k t e -> p k e t"),
                 )
-                piece_grouped[u] = grouped[:, 0 : 2 * HEAD, :].rearrange("p w t -> p (w t)")
 
-        def regroup_piece_via_tensor(u, copy):
-            grouped = stage.tile([P, BANK, PACK], BF16, align_bytes=64, name="grouped")
-            flat = grouped[:].rearrange("p w t -> p (w t)")
+        def regroup_half(u, half, engine):
+            columns = slice(BANK // 2 * half, BANK // 2 * (half + 1))
+            if half == 0:
+                piece_grouped[u] = new_group(lone_stage)
+            regroup(engine, piece_grouped[u][:, columns, :], piece_rows[u][:, :, columns])
+
+        def regroup_piece_via_tensor(u):
+            piece_grouped[u] = new_group(stage)
             columns = BANK // PACK
             for half in range(2):
                 bank = shared_banks.tile([P, BF16_BANK], BF16, tag="bank", name="bank")
@@ -172,8 +190,17 @@ def tile_transformerlayer_pa_kernel(
                         start=True,
                         stop=True,
                     )
-                copy(out=flat[:, BF16_BANK * half : BF16_BANK * (half + 1)], in_=bank[:])
-            piece_grouped[u] = flat
+                nc.scalar.copy(
+                    out=piece_grouped[u][:].rearrange("p w t -> p (w t)")[
+                        :, BF16_BANK * half : BF16_BANK * (half + 1)
+                    ],
+                    in_=bank[:],
+                )
+
+        def quantise(grouped, codes, scales):
+            nc.vector.quantize_mx(
+                out=codes.bitcast(FP8X4), scales=scales, in_=grouped.rearrange("p w t -> p (w t)")
+            )
 
         def quantise_piece(u):
             b, g = divmod(u, PASSES)
@@ -181,7 +208,9 @@ def tile_transformerlayer_pa_kernel(
             if g == 0:
                 block_codes[b] = quantised.tile([P, PASSES, BANK], U32, name="w_codes", align_bytes=64)
                 block_scales[b] = quantised.tile([P, PASSES, BANK], U8, name="w_scales", align_bytes=64)
-            quantise(piece_grouped[u], block_codes[b][:, g, :width], block_scales[b][:, g, :width])
+            quantise(
+                piece_grouped[u][:, 0:width, :], block_codes[b][:, g, 0:width], block_scales[b][:, g, 0:width]
+            )
 
         stats = [small.tile([P, CHUNKS, 6], F32, name="stats") for i in range(TOKEN_TILES)]
         mean_var = [small.tile([P, 2], F32, name="mean_var") for i in range(TOKEN_TILES)]
@@ -204,44 +233,32 @@ def tile_transformerlayer_pa_kernel(
             nc.vector.tensor_scalar_mul(out=minus_mean[i][:], in0=mean_var[i][:, 0:1], scalar1=-1.0)
             nc.gpsimd.tensor_tensor(out=rstd[i][:], in0=var_eps[:], in1=minus_half[:], op=ALU.pow)
 
+        def in_order(i):
+            return x_sb[i][:].rearrange("p (g q t) -> p g t q", q=P, t=PACK)
+
+        def in_squares(i):
+            return normed[i][:].rearrange("p (g t q) -> p g t q", q=P, t=PACK)
+
         def normalise_on_scalar(i):
             shift = small.tile([P, 1], F32, name="shift")
             nc.gpsimd.tensor_tensor(out=shift[:], in0=minus_mean[i][:], in1=rstd[i][:], op=ALU.mult)
             nc.scalar.activation(
-                out=normed[i][:].rearrange("p (g t q) -> p g t q", q=P, t=PACK),
-                in_=x_sb[i][:].rearrange("p (g q t) -> p g t q", q=P, t=PACK),
-                func=ACT.Identity,
-                scale=rstd[i][:],
-                bias=shift[:],
+                out=in_squares(i), in_=in_order(i), func=ACT.Identity, scale=rstd[i][:], bias=shift[:]
             )
 
         def normalise(i, engine, passes=slice(0, PASSES)):
             engine.tensor_scalar(
-                out=normed[i][:].rearrange("p (g t q) -> p g t q", q=P, t=PACK)[:, passes],
-                in0=x_sb[i][:].rearrange("p (g q t) -> p g t q", q=P, t=PACK)[:, passes],
+                out=in_squares(i)[:, passes],
+                in0=in_order(i)[:, passes],
                 scalar1=minus_mean[i][:],
                 scalar2=rstd[i][:],
                 op0=ALU.add,
                 op1=ALU.mult,
             )
 
+        for u in range(3):
+            regroup_piece(u, "scalar")
         take_stats(0, range(CHUNKS))
-        regroup_piece(0, nc.scalar.copy)
-        regroup_piece(1, nc.scalar.copy)
-        regroup_piece(2, nc.scalar.copy)
-        heads_a_bank = BF16_BANK // HEAD
-        bias_banks = []
-        for first in range(0, HEADS, heads_a_bank):
-            bias_bank = even_sums.tile([P, BF16_BANK], BF16, tag="bank", name="bank")
-            bias_banks.append(bias_bank)
-            for r in range(first, min(first + heads_a_bank, HEADS)):
-                nc.tensor.matmul(
-                    out=bias_bank[:, HEAD * (r - first) : HEAD * (r - first + 1)],
-                    lhsT=identity_bf16[:, r : r + 1].to_broadcast([P, P]),
-                    rhs=small_rows[:, PASS_D:],
-                    start=True,
-                    stop=True,
-                )
         for i in range(1, TOKEN_TILES):
             take_stats(i, range(1))
             aggregate(i - 1)
@@ -256,36 +273,38 @@ def tile_transformerlayer_pa_kernel(
         aggregate(3)
         normalise(2, nc.vector, slice(2, 4))
         take_rstd(3)
+        gain_cols = keep.tile([P, 2 * PASSES, PACK], F32, name="gain_cols")
         nc.vector.tensor_copy(
             out=gain_cols[:], in_=gain_bank[:, :, 0 : 2 * PASSES].rearrange("p t r -> p r t")
         )
+        bias_all = keep.tile([P, HEAD * HEADS], BF16, name="bias_all")
         for c in range(len(bias_banks)):
             columns = min(BF16_BANK, HEAD * HEADS - BF16_BANK * c)
             nc.vector.tensor_copy(
-                out=bias_all[:, BF16_BANK * c : BF16_BANK * c + columns], in_=bias_banks[c][:, :columns]
+                out=bias_all[:, BF16_BANK * c : BF16_BANK * c + columns], in_=bias_banks[c][:, 0:columns]
             )
         normalise(3, nc.vector)
         quantise_piece(0)
-        regroup_piece_via_tensor(3, nc.scalar.copy)
-        regroup_piece_via_tensor(4, nc.scalar.copy)
+        regroup_piece_via_tensor(3)
+        regroup_piece_via_tensor(4)
 
+        h_codes = keep.tile([P, PASSES, TOKENS], U32, name="h_codes", align_bytes=64)
+        h_scales = keep.tile([P, PASSES, TOKENS], U8, name="h_scales", align_bytes=64)
         block_sums = {}
 
         def multiply_piece(u):
             b, g = divmod(u, PASSES)
             width = block_width(b)
             if g == 0:
-                pool = shared_banks if b % 2 else even_sums
-                block_sums[b] = [
-                    pool.tile([P, BANK], F32, tag="bank", name="bank") for i in range(TOKEN_TILES)
-                ]
+                pool = shared_banks if b % 2 else even_banks
+                block_sums[b] = [pool.tile([P, BANK], F32, tag="bank", name="bank") for i in range(TOKEN_TILES)]
             for i in range(TOKEN_TILES):
                 nc.tensor.matmul_mx(
-                    out=block_sums[b][i][:, :width],
+                    out=block_sums[b][i][:, 0:width],
                     lhsT=h_codes[:, g, P * i : P * (i + 1)].bitcast(FP8X4),
                     lhsT_scale=h_scales[:, g, P * i : P * (i + 1)],
-                    rhs=block_codes[b][:, g, :width].bitcast(FP8X4),
-                    rhs_scale=block_scales[b][:, g, :width],
+                    rhs=block_codes[b][:, g, 0:width].bitcast(FP8X4),
+                    rhs_scale=block_scales[b][:, g, 0:width],
                     start=(g == 0),
                     stop=(g == PASSES - 1),
                 )
@@ -295,8 +314,8 @@ def tile_transformerlayer_pa_kernel(
             for i in range(TOKEN_TILES):
                 result = results.tile([P, BANK], F32, name="result")
                 nc.vector.tensor_tensor(
-                    out=result[:, :width],
-                    in0=block_sums[b][i][:, :width],
+                    out=result[:, 0:width],
+                    in0=block_sums[b][i][:, 0:width],
                     in1=bias_all[:, BANK * b : BANK * b + width],
                     op=ALU.add,
                 )
@@ -307,13 +326,9 @@ def tile_transformerlayer_pa_kernel(
                     nc.sync.dma_start(out=v_tiles[i], in_=result[:, HEAD : 2 * HEAD])
 
         h_rows = keep.tile([P, D_SQUARES, TOKENS], BF16, name="h_rows")
-        h_codes = keep.tile([P, PASSES, TOKENS], U32, name="h_codes", align_bytes=64)
-        h_scales = keep.tile([P, PASSES, TOKENS], U8, name="h_scales", align_bytes=64)
-
-        gain_flat = gain_cols[:].rearrange("p r t -> p (r t)")
-
-        def transpose_pass(g):
-            for j in range(PACK * g, PACK * (g + 1)):
+        for g in range(PASSES):
+            for t in range(PACK):
+                j = PACK * g + t
                 square = shared_banks.tile([P, BANK], F32, tag="bank", name="bank")
                 for i in range(TOKEN_TILES):
                     nc.tensor.transpose(
@@ -323,40 +338,41 @@ def tile_transformerlayer_pa_kernel(
                     out=h_rows[:, j, :],
                     in_=square[:],
                     func=ACT.Identity,
-                    scale=gain_flat[:, j : j + 1],
-                    bias=gain_flat[:, D_SQUARES + j : D_SQUARES + j + 1],
+                    scale=gain_cols[:, g, t : t + 1],
+                    bias=gain_cols[:, PASSES + g, t : t + 1],
                 )
 
-        def regroup_pass(g):
-            return regroup(h_stage, nc.vector.tensor_copy, h_rows[:, PACK * g : PACK * (g + 1), :])
-
-        def quantise_pass(g, h_grouped):
-            quantise(h_grouped, h_codes[:, g, :], h_scales[:, g, :])
-
-        transpose_pass(0)
-        transpose_pass(1)
-        transpose_pass(2)
-        transpose_pass(3)
         quantise_piece(1)
-        regroup_piece(5, nc.vector.tensor_copy)
+        regroup_piece(5, "vector")
         quantise_piece(2)
-        regroup_piece(6, nc.vector.tensor_copy)
+        regroup_piece(6, "vector")
         for g in range(PASSES):
-            h_grouped = regroup_pass(g)
+            h_grouped = new_group(h_stage)
+            regroup("vector", h_grouped[:], h_rows[:, PACK * g : PACK * (g + 1), :])
             quantise_piece(g + 3)
-            quantise_pass(g, h_grouped)
+            quantise(h_grouped[:], h_codes[:, g, :], h_scales[:, g, :])
             multiply_piece(g)
-        regroup_piece(7, nc.scalar.copy)
-        regroup_piece(8, nc.scalar.copy)
 
+        regroup_piece(7, "scalar", lone_stage)
+        regroup_piece(8, "vector")
         for u in range(PASSES, PIECES):
             b, g = divmod(u, PASSES)
-            if u > 6:
+            if u > PASSES + 2:
                 quantise_piece(u)
-            ahead = u + 4
-            if 8 < ahead < PIECES:
-                regroup_piece(ahead, gpsimd_copy if ahead in (9, 13, 17) else (nc.vector.tensor_copy if ahead in (10, 18,) else nc.scalar.copy))
+            ahead = u + AHEAD
+            if ahead == PIECES - 3:
+                regroup_piece(ahead, "gpsimd", lone_stage)
+            elif ahead > 8 and ahead not in (9, 13) and ahead < PIECES:
+                regroup_piece(ahead, "scalar")
             multiply_piece(u)
-            if u in (7, 10, 13, 18):
+            if u == 7:
+                regroup_half(9, 0, "gpsimd")
+                finish_block(0)
+                regroup_half(9, 1, "vector")
+            elif u == 10:
+                regroup_half(13, 0, "gpsimd")
+                finish_block(1)
+                regroup_half(13, 1, "vector")
+            elif u > 10 and g == 2:
                 finish_block(b - 1)
         finish_block(BLOCKS - 1)

@@ -34,7 +34,8 @@ BLOCKS = Q_BLOCKS + 1
 PIECES = BLOCKS * PASSES
 AHEAD = 4
 GROUPED_BUFS = 6
-RUN = {"vector": 2, "scalar": 4, "gpsimd": 1}
+RUN = {"vector": 2, "scalar": 1, "gpsimd": 1}
+GPSIMD_COLS = 320
 
 FLOPS = 2 * TOKENS * D * HEADS * HEAD
 
@@ -120,7 +121,9 @@ def tile_transformerlayer_pa_kernel(
             x_i = keep.tile([P, D], BF16, name="x%d" % i)
             nc.sync.dma_start(out=x_i[:], in_=x_tiles[i])
             x_sb.append(x_i)
-            load_pieces([0], i)
+            if i > 0:
+                load_pieces([0], i - 1)
+        load_pieces([0], PASSES - 1)
         for g in range(PASSES):
             load_pieces([1], g)
         for g in range(PASSES):
@@ -170,11 +173,12 @@ def tile_transformerlayer_pa_kernel(
                     kv_rows[:, :, g].rearrange("p k t e -> p k e t"),
                 )
 
-        def regroup_half(u, half, engine):
-            columns = slice(BANK // 2 * half, BANK // 2 * (half + 1))
-            if half == 0:
-                piece_grouped[u] = new_group(lone_stage)
-            regroup(engine, piece_grouped[u][:, columns, :], piece_rows[u][:, :, columns])
+        def regroup_first_part(u):
+            piece_grouped[u] = new_group(lone_stage)
+            regroup("gpsimd", piece_grouped[u][:, 0:GPSIMD_COLS, :], piece_rows[u][:, :, 0:GPSIMD_COLS])
+
+        def regroup_rest(u):
+            regroup("vector", piece_grouped[u][:, GPSIMD_COLS:, :], piece_rows[u][:, :, GPSIMD_COLS:])
 
         def regroup_piece_via_tensor(u):
             piece_grouped[u] = new_group(stage)
@@ -366,13 +370,13 @@ def tile_transformerlayer_pa_kernel(
                 regroup_piece(ahead, "scalar")
             multiply_piece(u)
             if u == 7:
-                regroup_half(9, 0, "gpsimd")
+                regroup_first_part(9)
                 finish_block(0)
-                regroup_half(9, 1, "vector")
+                regroup_rest(9)
             elif u == 10:
-                regroup_half(13, 0, "gpsimd")
+                regroup_first_part(13)
                 finish_block(1)
-                regroup_half(13, 1, "vector")
+                regroup_rest(13)
             elif u > 10 and g == 2:
                 finish_block(b - 1)
         finish_block(BLOCKS - 1)

@@ -119,7 +119,10 @@ def tile_transformerlayer_pa_kernel(
         x_sb = []
         for i in range(TOKEN_TILES):
             x_i = keep.tile([P, D], BF16, name="x%d" % i)
-            nc.sync.dma_start(out=x_i[:], in_=x_tiles[i])
+            loads = 2 if i == 0 else 1
+            for c in range(loads):
+                columns = slice(D // loads * c, D // loads * (c + 1))
+                nc.sync.dma_start(out=x_i[:, columns], in_=x_tiles[i][:, columns])
             x_sb.append(x_i)
             if i > 0:
                 load_pieces([0], i - 1)
@@ -313,9 +316,9 @@ def tile_transformerlayer_pa_kernel(
                     stop=(g == PASSES - 1),
                 )
 
-        def finish_block(b):
+        def finish_block(b, tiles=range(TOKEN_TILES)):
             width = block_width(b)
-            for i in range(TOKEN_TILES):
+            for i in tiles:
                 result = results.tile([P, BANK], F32, name="result")
                 nc.vector.tensor_tensor(
                     out=result[:, 0:width],
@@ -377,6 +380,9 @@ def tile_transformerlayer_pa_kernel(
                 regroup_first_part(13)
                 finish_block(1)
                 regroup_rest(13)
-            elif u > 10 and g == 2:
-                finish_block(b - 1)
-        finish_block(BLOCKS - 1)
+            elif u == 14:
+                finish_block(2)
+            elif u == 18:
+                finish_block(3, range(TOKEN_TILES - 1))
+        finish_block(3, range(TOKEN_TILES - 1, TOKEN_TILES))
+        finish_block(4)

from contextlib import ExitStack

import concourse.mybir as mybir
from concourse.masks import make_identity

F32 = mybir.dt.float32
BF16 = mybir.dt.bfloat16
U32 = mybir.dt.uint32
U8 = mybir.dt.uint8
FP8X4 = mybir.dt.float8_e4m3fn_x4
ALU = mybir.AluOpType
ACT = mybir.ActivationFunctionType

P = 128
PACK = 4
TOKENS = 512
D = 2048
HEAD = 128
Q_HEADS = 16
HEADS = Q_HEADS + 2
EPS = 1e-05

TOKEN_TILES = TOKENS // P
D_SQUARES = D // P
PASS_D = P * PACK
PASSES = D // PASS_D
BANK = 512
BF16_BANK = 2 * BANK
STATS_CHUNK = 512
CHUNKS = D // STATS_CHUNK

Q_BLOCKS = Q_HEADS * HEAD // BANK
BLOCKS = Q_BLOCKS + 1
PIECES = BLOCKS * PASSES
AHEAD = 4
GROUPED_BUFS = 6
RUN = {"vector": 2, "scalar": 1, "gpsimd": 1}
GPSIMD_COLS = 320

FLOPS = 2 * TOKENS * D * HEADS * HEAD


def tile_transformerlayer_pa_kernel(
    tc, x, ln1_s, ln1_b, wq_k, wq_b, wk_k, wk_b, wv_k, wv_b, out_0, out_1, out_2
):
    nc = tc.nc

    x_tiles = x.rearrange("b (i p) d -> (b i) p d", p=P)
    wq_rows = wq_k.rearrange("(g p t) h e -> g p t (h e)", p=P, t=PACK)
    wk_rows = wk_k.rearrange("(g p t) e -> p g (t e)", p=P, t=PACK)
    wv_rows = wv_k.rearrange("(g p t) e -> p g (t e)", p=P, t=PACK)
    q_tiles = out_0.rearrange("b (i p) h e -> (b i) p (h e)", p=P)
    k_tiles = out_1.rearrange("b (i p) e -> (b i) p e", p=P)
    v_tiles = out_2.rearrange("b (i p) e -> (b i) p e", p=P)

    with ExitStack() as ctx:
        ctx.enter_context(tc.manual_schedule())
        keep = ctx.enter_context(tc.tile_pool(name="keep", bufs=1))
        small = ctx.enter_context(tc.tile_pool(name="small", bufs=TOKEN_TILES))
        loaded = ctx.enter_context(tc.tile_pool(name="loaded", bufs=1))
        stage = ctx.enter_context(tc.tile_pool(name="stage", bufs=GROUPED_BUFS))
        lone_stage = ctx.enter_context(tc.tile_pool(name="lone_stage", bufs=1))
        h_stage = ctx.enter_context(tc.tile_pool(name="h_stage", bufs=2))
        quantised = ctx.enter_context(tc.tile_pool(name="quantised", bufs=3))
        results = ctx.enter_context(tc.tile_pool(name="results", bufs=8))
        even_banks = ctx.enter_context(tc.psum_pool(name="even_banks", bufs=TOKEN_TILES))
        shared_banks = ctx.enter_context(tc.psum_pool(name="shared_banks", bufs=TOKEN_TILES))

        minus_half = keep.tile([P, 1], F32, name="minus_half")
        nc.vector.memset(minus_half[:], -0.5)
        warm = keep.tile([P, 1], F32, name="warm")
        nc.scalar.activation(out=warm[:], in_=minus_half[:], func=ACT.Identity)

        small_rows = keep.tile([P, PASS_D + HEAD], BF16, name="small_rows")
        nc.vector.memset(small_rows[:], 0.0)
        nc.scalar.dma_start(out=small_rows[0:PASSES, 0:PASS_D], in_=ln1_s.rearrange("(g d) -> g d", d=PASS_D))
        nc.scalar.dma_start(
            out=small_rows[PASSES : 2 * PASSES, 0:PASS_D], in_=ln1_b.rearrange("(g d) -> g d", d=PASS_D)
        )
        nc.scalar.dma_start(out=small_rows[0:Q_HEADS, PASS_D:], in_=wq_b)
        nc.scalar.dma_start(
            out=small_rows[Q_HEADS : Q_HEADS + 1, PASS_D:], in_=wk_b.rearrange("(a e) -> a e", a=1)
        )
        nc.scalar.dma_start(
            out=small_rows[Q_HEADS + 1 : Q_HEADS + 2, PASS_D:], in_=wv_b.rearrange("(a e) -> a e", a=1)
        )
        identity = keep.tile([P, P], F32, name="identity")
        make_identity(nc, identity[:])
        identity_bf16 = keep.tile([P, P], BF16, name="identity_bf16")
        nc.vector.tensor_copy(out=identity_bf16[:], in_=identity[:])

        gain_bank = even_banks.tile([P, PACK, P], BF16, tag="bank", name="bank")
        for t in range(PACK):
            nc.tensor.transpose(gain_bank[:, t, :], small_rows[:, t:PASS_D:PACK], identity_bf16[:])

        heads_a_bank = BF16_BANK // HEAD
        bias_banks = []
        for first in range(0, HEADS, heads_a_bank):
            bias_bank = even_banks.tile([P, BF16_BANK], BF16, tag="bank", name="bank")
            bias_banks.append(bias_bank)
            for r in range(first, min(first + heads_a_bank, HEADS)):
                nc.tensor.matmul(
                    out=bias_bank[:, HEAD * (r - first) : HEAD * (r - first + 1)],
                    lhsT=identity_bf16[:, r : r + 1].to_broadcast([P, P]),
                    rhs=small_rows[:, PASS_D:],
                    start=True,
                    stop=True,
                )

        piece_rows = {}

        def load_pieces(blocks, g):
            first, last = BANK * blocks[0], BANK * (blocks[-1] + 1)
            rows = loaded.tile([P, PACK, last - first], BF16, name="rows%d_%d" % (blocks[0], g))
            nc.sync.dma_start(out=rows[:], in_=wq_rows[g][:, :, first:last])
            for b in blocks:
                piece_rows[PASSES * b + g] = rows[:, :, BANK * b - first : BANK * (b + 1) - first]

        x_sb = []
        for i in range(TOKEN_TILES):
            x_i = keep.tile([P, D], BF16, name="x%d" % i)
            loads = 2 if i == 0 else 1
            for c in range(loads):
                columns = slice(D // loads * c, D // loads * (c + 1))
                nc.sync.dma_start(out=x_i[:, columns], in_=x_tiles[i][:, columns])
            x_sb.append(x_i)
            if i > 0:
                load_pieces([0], i - 1)
        load_pieces([0], PASSES - 1)
        for g in range(PASSES):
            load_pieces([1], g)
        for g in range(PASSES):
            load_pieces([2, 3], g)
        kv_rows = loaded.tile([P, 2, PASSES, PACK, HEAD], BF16, name="kv_rows")
        nc.sync.dma_start(out=kv_rows[:, 0].rearrange("p g t e -> p g (t e)"), in_=wk_rows)
        nc.sync.dma_start(out=kv_rows[:, 1].rearrange("p g t e -> p g (t e)"), in_=wv_rows)

        def copy_on(engine, out, in_):
            if engine == "vector":
                nc.vector.tensor_copy(out=out, in_=in_)
            elif engine == "scalar":
                nc.scalar.copy(out=out, in_=in_)
            else:
                nc.gpsimd.tensor_scalar(out=out, in0=in_, scalar1=1.0, scalar2=0.0, op0=ALU.mult, op1=ALU.add)

        def regroup(engine, grouped, rows):
            run = RUN[engine]
            if run == 1:
                copy_on(engine, grouped, rows.rearrange("p t c -> p c t"))
            else:
                copy_on(
                    engine,
                    grouped.rearrange("p (c i) t -> p c t i", i=run),
                    rows.rearrange("p t (c i) -> p c t i", i=run),
                )

        def new_group(pool):
            return pool.tile([P, BANK, PACK], BF16, align_bytes=64, name="grouped")

        def block_width(b):
            return BANK if b < Q_BLOCKS else 2 * HEAD

        piece_grouped = {}
        block_codes = {}
        block_scales = {}

        def regroup_piece(u, engine, pool=stage):
            b, g = divmod(u, PASSES)
            piece_grouped[u] = new_group(pool)
            if b < Q_BLOCKS:
                regroup(engine, piece_grouped[u][:], piece_rows[u])
            else:
                copy_on(
                    engine,
                    piece_grouped[u][:, 0 : 2 * HEAD, :].rearrange("p (k e) t -> p k e t", k=2),
                    kv_rows[:, :, g].rearrange("p k t e -> p k e t"),
                )

        def regroup_first_part(u):
            piece_grouped[u] = new_group(lone_stage)
            regroup("gpsimd", piece_grouped[u][:, 0:GPSIMD_COLS, :], piece_rows[u][:, :, 0:GPSIMD_COLS])

        def regroup_rest(u):
            regroup("vector", piece_grouped[u][:, GPSIMD_COLS:, :], piece_rows[u][:, :, GPSIMD_COLS:])

        def regroup_piece_via_tensor(u):
            piece_grouped[u] = new_group(stage)
            columns = BANK // PACK
            for half in range(2):
                bank = shared_banks.tile([P, BF16_BANK], BF16, tag="bank", name="bank")
                for c in range(2):
                    first = columns * (2 * half + c)
                    nc.tensor.matmul(
                        out=bank[:, BANK * c : BANK * (c + 1)].rearrange("p (w t) -> p t w", t=PACK),
                        lhsT=identity_bf16[:],
                        rhs=piece_rows[u][:, :, first : first + columns],
                        start=True,
                        stop=True,
                    )
                nc.scalar.copy(
                    out=piece_grouped[u][:].rearrange("p w t -> p (w t)")[
                        :, BF16_BANK * half : BF16_BANK * (half + 1)
                    ],
                    in_=bank[:],
                )

        def quantise(grouped, codes, scales):
            nc.vector.quantize_mx(
                out=codes.bitcast(FP8X4), scales=scales, in_=grouped.rearrange("p w t -> p (w t)")
            )

        def quantise_piece(u):
            b, g = divmod(u, PASSES)
            width = block_width(b)
            if g == 0:
                block_codes[b] = quantised.tile([P, PASSES, BANK], U32, name="w_codes", align_bytes=64)
                block_scales[b] = quantised.tile([P, PASSES, BANK], U8, name="w_scales", align_bytes=64)
            quantise(
                piece_grouped[u][:, 0:width, :], block_codes[b][:, g, 0:width], block_scales[b][:, g, 0:width]
            )

        stats = [small.tile([P, CHUNKS, 6], F32, name="stats") for i in range(TOKEN_TILES)]
        mean_var = [small.tile([P, 2], F32, name="mean_var") for i in range(TOKEN_TILES)]
        minus_mean = [small.tile([P, 1], F32, name="minus_mean") for i in range(TOKEN_TILES)]
        rstd = [small.tile([P, 1], F32, name="rstd") for i in range(TOKEN_TILES)]
        normed = [keep.tile([P, D], F32, name="normed%d" % i) for i in range(TOKEN_TILES)]

        def take_stats(i, chunks):
            for c in chunks:
                nc.vector.bn_stats(
                    out=stats[i][:, c, :], in_=x_sb[i][:, STATS_CHUNK * c : STATS_CHUNK * (c + 1)]
                )

        def aggregate(i):
            nc.vector.bn_aggr(out=mean_var[i][:], in_=stats[i][:].rearrange("p c s -> p (c s)"))

        def take_rstd(i):
            var_eps = small.tile([P, 1], F32, name="var_eps")
            nc.vector.tensor_scalar_add(out=var_eps[:], in0=mean_var[i][:, 1:2], scalar1=EPS)
            nc.vector.tensor_scalar_mul(out=minus_mean[i][:], in0=mean_var[i][:, 0:1], scalar1=-1.0)
            nc.gpsimd.tensor_tensor(out=rstd[i][:], in0=var_eps[:], in1=minus_half[:], op=ALU.pow)

        def in_order(i):
            return x_sb[i][:].rearrange("p (g q t) -> p g t q", q=P, t=PACK)

        def in_squares(i):
            return normed[i][:].rearrange("p (g t q) -> p g t q", q=P, t=PACK)

        def normalise_on_scalar(i):
            shift = small.tile([P, 1], F32, name="shift")
            nc.gpsimd.tensor_tensor(out=shift[:], in0=minus_mean[i][:], in1=rstd[i][:], op=ALU.mult)
            nc.scalar.activation(
                out=in_squares(i), in_=in_order(i), func=ACT.Identity, scale=rstd[i][:], bias=shift[:]
            )

        def normalise(i, engine, passes=slice(0, PASSES)):
            engine.tensor_scalar(
                out=in_squares(i)[:, passes],
                in0=in_order(i)[:, passes],
                scalar1=minus_mean[i][:],
                scalar2=rstd[i][:],
                op0=ALU.add,
                op1=ALU.mult,
            )

        for u in range(3):
            regroup_piece(u, "scalar")
        take_stats(0, range(CHUNKS))
        for i in range(1, TOKEN_TILES):
            take_stats(i, range(1))
            aggregate(i - 1)
            take_stats(i, range(1, 2))
            take_rstd(i - 1)
            if i == 1:
                normalise(0, nc.gpsimd)
            if i == 2:
                normalise_on_scalar(1)
            take_stats(i, range(2, CHUNKS))
        normalise(2, nc.vector, slice(0, 2))
        aggregate(3)
        normalise(2, nc.vector, slice(2, 4))
        take_rstd(3)
        gain_cols = keep.tile([P, 2 * PASSES, PACK], F32, name="gain_cols")
        nc.vector.tensor_copy(
            out=gain_cols[:], in_=gain_bank[:, :, 0 : 2 * PASSES].rearrange("p t r -> p r t")
        )
        bias_all = keep.tile([P, HEAD * HEADS], BF16, name="bias_all")
        for c in range(len(bias_banks)):
            columns = min(BF16_BANK, HEAD * HEADS - BF16_BANK * c)
            nc.vector.tensor_copy(
                out=bias_all[:, BF16_BANK * c : BF16_BANK * c + columns], in_=bias_banks[c][:, 0:columns]
            )
        normalise(3, nc.vector)
        quantise_piece(0)
        regroup_piece_via_tensor(3)
        regroup_piece_via_tensor(4)

        h_codes = keep.tile([P, PASSES, TOKENS], U32, name="h_codes", align_bytes=64)
        h_scales = keep.tile([P, PASSES, TOKENS], U8, name="h_scales", align_bytes=64)
        block_sums = {}

        def multiply_piece(u):
            b, g = divmod(u, PASSES)
            width = block_width(b)
            if g == 0:
                pool = shared_banks if b % 2 else even_banks
                block_sums[b] = [pool.tile([P, BANK], F32, tag="bank", name="bank") for i in range(TOKEN_TILES)]
            for i in range(TOKEN_TILES):
                nc.tensor.matmul_mx(
                    out=block_sums[b][i][:, 0:width],
                    lhsT=h_codes[:, g, P * i : P * (i + 1)].bitcast(FP8X4),
                    lhsT_scale=h_scales[:, g, P * i : P * (i + 1)],
                    rhs=block_codes[b][:, g, 0:width].bitcast(FP8X4),
                    rhs_scale=block_scales[b][:, g, 0:width],
                    start=(g == 0),
                    stop=(g == PASSES - 1),
                )

        def finish_block(b, tiles=range(TOKEN_TILES)):
            width = block_width(b)
            for i in tiles:
                result = results.tile([P, BANK], F32, name="result")
                nc.vector.tensor_tensor(
                    out=result[:, 0:width],
                    in0=block_sums[b][i][:, 0:width],
                    in1=bias_all[:, BANK * b : BANK * b + width],
                    op=ALU.add,
                )
                if b < Q_BLOCKS:
                    nc.sync.dma_start(out=q_tiles[i][:, BANK * b : BANK * (b + 1)], in_=result[:])
                else:
                    nc.sync.dma_start(out=k_tiles[i], in_=result[:, 0:HEAD])
                    nc.sync.dma_start(out=v_tiles[i], in_=result[:, HEAD : 2 * HEAD])

        h_rows = keep.tile([P, D_SQUARES, TOKENS], BF16, name="h_rows")
        for g in range(PASSES):
            for t in range(PACK):
                j = PACK * g + t
                square = shared_banks.tile([P, BANK], F32, tag="bank", name="bank")
                for i in range(TOKEN_TILES):
                    nc.tensor.transpose(
                        square[:, P * i : P * (i + 1)], normed[i][:, P * j : P * (j + 1)], identity[:]
                    )
                nc.scalar.activation(
                    out=h_rows[:, j, :],
                    in_=square[:],
                    func=ACT.Identity,
                    scale=gain_cols[:, g, t : t + 1],
                    bias=gain_cols[:, PASSES + g, t : t + 1],
                )

        quantise_piece(1)
        regroup_piece(5, "vector")
        quantise_piece(2)
        regroup_piece(6, "vector")
        for g in range(PASSES):
            h_grouped = new_group(h_stage)
            regroup("vector", h_grouped[:], h_rows[:, PACK * g : PACK * (g + 1), :])
            quantise_piece(g + 3)
            quantise(h_grouped[:], h_codes[:, g, :], h_scales[:, g, :])
            multiply_piece(g)

        regroup_piece(7, "scalar", lone_stage)
        regroup_piece(8, "vector")
        for u in range(PASSES, PIECES):
            b, g = divmod(u, PASSES)
            if u > PASSES + 2:
                quantise_piece(u)
            ahead = u + AHEAD
            if ahead == PIECES - 3:
                regroup_piece(ahead, "gpsimd", lone_stage)
            elif ahead > 8 and ahead not in (9, 13) and ahead < PIECES:
                regroup_piece(ahead, "scalar")
            multiply_piece(u)
            if u == 7:
                regroup_first_part(9)
                finish_block(0)
                regroup_rest(9)
            elif u == 10:
                regroup_first_part(13)
                finish_block(1)
                regroup_rest(13)
            elif u == 14:
                finish_block(2)
            elif u == 18:
                finish_block(3, range(TOKEN_TILES - 1))
        finish_block(3, range(TOKEN_TILES - 1, TOKEN_TILES))
        finish_block(4)
